import numpy as np
import ml_dtypes


def mxq(x, axis, fmt="e4m3"):
    dtype, down = {"e4m3": (ml_dtypes.float8_e4m3fn, 7), "e5m2": (ml_dtypes.float8_e5m2, 14)}[fmt]
    v = np.moveaxis(np.asarray(x, np.float32).astype(ml_dtypes.bfloat16).astype(np.float64), axis, -1)
    blocks = v.reshape(v.shape[:-1] + (-1, 32))
    amax = np.abs(blocks).max(-1, keepdims=True)
    byte = np.maximum(np.where(amax > 0, np.frexp(amax)[1] - 1 + 127, 0) - down, 1)
    scale = np.exp2(byte - 127.0)
    codes = (blocks / scale).astype(np.float32).astype(dtype).astype(np.float64)
    return np.moveaxis((codes * scale).reshape(v.shape), -1, axis)


WIDE = False


def mx_kscale(k):
    if not WIDE:
        return np.ones(k)
    levels = np.array([10, -10, 5, -5, 0])
    a = np.random.permutation(np.resize(levels, k // 512 * 4)).reshape(k // 512, 4)
    idx = np.arange(k)
    return np.exp2(a[idx // 512, idx % 128 // 32])


BF16 = ml_dtypes.bfloat16


def bf(x):
    return np.asarray(x, np.float32).astype(BF16)


def f64(x):
    return np.asarray(x).astype(np.float64)


E2M1 = np.array([0.0, 0.5, 1.0, 1.5, 2.0, 3.0, 4.0, 6.0, -0.0, -0.5, -1.0, -1.5, -2.0, -3.0, -4.0, -6.0])


def pack_weight(w, fmt):
    k, n = w.shape
    w = f64(bf(w)).reshape(k // 32, 32, n)
    amax = np.abs(w).max(1)
    if fmt == "e4m3":
        byte = np.frexp(amax)[1] - 1 + 127 - 7
    else:
        mant, ex = np.frexp(amax / 6.0)
        byte = np.where(mant > 0.5, ex, ex - 1) + 127
    byte = np.clip(np.where(amax > 0, byte, 1), 1, 254)
    scaled = (w * np.exp2(127.0 - byte)[:, None, :]).reshape(k, n).astype(np.float32)
    by_word = np.ascontiguousarray(scaled.reshape(k // 512, 128, 4, n).transpose(0, 1, 3, 2))
    if fmt == "e4m3":
        words = by_word.astype(ml_dtypes.float8_e4m3fn).view(np.uint8)
    else:
        c = by_word.astype(ml_dtypes.float4_e2m1fn).view(np.uint8) & 0xF
        words = c[..., 0::2] | (c[..., 1::2] << 4)
    return np.ascontiguousarray(words), np.ascontiguousarray(byte.astype(np.uint8).reshape(k // 512, 16, n))


def unpack_weight(words, scales, fmt):
    g, p, n, _ = words.shape
    if fmt == "e4m3":
        vals = np.ascontiguousarray(words).view(ml_dtypes.float8_e4m3fn).astype(np.float64)
    else:
        nib = np.empty((g, p, n, 4), np.uint8)
        nib[..., 0::2] = words & 0xF
        nib[..., 1::2] = words >> 4
        vals = E2M1[nib]
    vals = vals * np.repeat(np.exp2(scales.astype(np.float64) - 127.0), 8, axis=1)[..., None]
    return vals.transpose(0, 1, 3, 2).reshape(g * 512, n)


P, D, B = 3, 512, 1536
LAMBDA = 0.1
JJ, II = np.nonzero(1 - np.eye(P, dtype=np.int64))


def setup_inputs():
    s = mx_kscale(D)
    s = s / s.max()
    F = bf(np.random.standard_normal((P, D, B)) * s[:, None])
    R = np.random.standard_normal((P, P, D, D)) / np.sqrt(D * (P - 1)) / s
    cat = np.ascontiguousarray(R.swapaxes(2, 3)).reshape(-1, D)
    words, scales = pack_weight(cat, "e4m3")
    return {"F": F, "R_words": words, "R_scales": scales}


def reference(F, R_words, R_scales):
    p = F.shape[0]
    Fq = mxq(f64(F), 1, "e4m3")
    Rq = unpack_weight(R_words, R_scales, "e4m3").reshape(P, P, D, D).swapaxes(2, 3)[II, JJ]
    Fi = Fq[II]
    agg = Rq.reshape(P, P - 1, D, D).transpose(0, 2, 1, 3).reshape(P, D, (P - 1) * D) @ Fi.reshape(P, (P - 1) * D, B)
    updated = (f64(F) + agg) / p
    M = np.zeros((P, P, D, B))
    M[II, JJ] = Rq @ Fi
    Dif = M - M.swapaxes(0, 1)
    loss = LAMBDA * 0.5 * np.sum(Dif * Dif)
    return updated, loss

@@ -1,0 +1,264 @@
+from contextlib import ExitStack
+
+import concourse.mybir as mybir
+
+BF16 = mybir.dt.bfloat16
+F32 = mybir.dt.float32
+I32 = mybir.dt.int32
+U32 = mybir.dt.uint32
+U8 = mybir.dt.uint8
+FP8X4 = mybir.dt.float8_e4m3fn_x4
+ALU = mybir.AluOpType
+ACT = mybir.ActivationFunctionType
+
+PATCHES = 3
+FEATURES = 512
+COLUMNS = 1536
+P = 128
+PACK = 4
+BANK = 512
+ROW_TILES = FEATURES // P
+BANKS = COLUMNS // BANK
+GROUPS = 8
+SCALE_ROWS = FEATURES // 32
+
+THIRD = 1.0 / 3.0
+LOSS_WEIGHT = 0.1 * 0.5 * 2.0
+
+LOAD_SPANS = ((0, 1), (1, BANKS))
+
+FLOPS = 2 * FEATURES * FEATURES * COLUMNS * 2 * PATCHES * (PATCHES - 1)
+BYTES = (
+    PATCHES * FEATURES * COLUMNS * (2 + 4)
+    + PATCHES * (PATCHES - 1) * (FEATURES * FEATURES + SCALE_ROWS * FEATURES)
+    + 4
+)
+
+
+def plus(i):
+    return i
+
+
+def minus(i):
+    return PATCHES + i - 1
+
+
+VERSIONS = 2 * PATCHES - 1
+
+
+def group(i, j):
+    return PATCHES * i + j
+
+
+def others(left_out):
+    return [i for i in range(PATCHES) if i != left_out]
+
+
+def load_span(bank):
+    for first, end in LOAD_SPANS:
+        if first <= bank < end:
+            return first * BANK, end * BANK
+    raise ValueError(bank)
+
+
+def tile_sheaflayer_t_e_kernel(tc, F, R_words, R_scales, out_0, out_1):
+    nc = tc.nc
+
+    rounds = [(bank, left_out) for bank in range(BANKS) for left_out in (2, 1, 0)]
+    steps = [(bank, i) for bank in range(BANKS) for i in range(PATCHES)]
+
+    with ExitStack() as ctx:
+        keep = ctx.enter_context(tc.tile_pool(name="keep", bufs=1))
+        stage = ctx.enter_context(tc.tile_pool(name="stage", bufs=3))
+        psum = ctx.enter_context(tc.psum_pool(name="psum", bufs=4))
+        ctx.enter_context(tc.manual_schedule())
+
+        raw_of = {}
+        resid_of = {}
+        for i in range(PATCHES):
+            for first_bank, end_bank in LOAD_SPANS:
+                first, width = first_bank * BANK, (end_bank - first_bank) * BANK
+                raw_of[(i, first)] = keep.tile([P, PACK, width], BF16, name="raw_%d_%d" % (i, first))
+                resid_of[(i, first)] = keep.tile(
+                    [P, ROW_TILES, width], BF16, name="resid_%d_%d" % (i, first)
+                )
+        result = keep.tile([P, PATCHES, ROW_TILES, COLUMNS], F32)
+        f_codes = keep.tile([P, VERSIONS, COLUMNS], U32, align_bytes=64)
+        f_scales = keep.tile([P, VERSIONS, COLUMNS], U8, align_bytes=64)
+        r_codes = keep.tile([P, GROUPS, FEATURES], U32, align_bytes=64)
+        r_scales = keep.tile([P, GROUPS, FEATURES], U8, align_bytes=64)
+        ones = keep.tile([P, P], F32)
+        square_sums = keep.tile([P, len(rounds) * ROW_TILES], F32)
+        loss_sum = keep.tile([P, 1], F32)
+        loss = keep.tile([P, 1], F32)
+
+        nc.vector.memset(r_scales[:].bitcast(I32), 0)
+        nc.vector.memset(ones[:], 1.0)
+
+        loaded = set()
+
+        def load_once(key, out, in_):
+            if key not in loaded:
+                loaded.add(key)
+                nc.sync.dma_start(out=out, in_=in_)
+
+        def load_raw(bank, i):
+            first, end = load_span(bank)
+            load_once(
+                ("raw", i, first),
+                raw_of[(i, first)][:],
+                F[i, :, first:end].rearrange("(p t) b -> p t b", t=PACK),
+            )
+
+        def load_weights(e):
+            for r in range(4):
+                load_once(
+                    ("scales", r),
+                    r_scales[r:P:32, :, :].bitcast(I32),
+                    R_scales[0:GROUPS, r:SCALE_ROWS:4, :].rearrange("g q n -> q g n").bitcast(I32),
+                )
+            load_once(
+                ("codes", e),
+                r_codes[:, e, :].bitcast(I32),
+                R_words[e].rearrange("p n t -> p (n t)").bitcast(I32),
+            )
+
+        def load_operands(bank, left_out):
+            i, j = others(left_out)
+            load_raw(bank, i)
+            load_raw(bank, j)
+            for e in (group(i, j), group(j, i), group(i, left_out), group(j, left_out)):
+                load_weights(e)
+
+        def load_residual(bank, left_out):
+            first, end = load_span(bank)
+            load_once(
+                ("resid", left_out, first),
+                resid_of[(left_out, first)][:],
+                F[left_out, :, first:end].rearrange("(m p) b -> p m b", p=P),
+            )
+
+        def third_of_residual(bank, left_out):
+            cols = slice(bank * BANK, (bank + 1) * BANK)
+            first, end = load_span(bank)
+            start = bank * BANK - first
+            for m in range(ROW_TILES):
+                nc.gpsimd.tensor_scalar(
+                    out=result[:, left_out, m, cols],
+                    in0=resid_of[(left_out, first)][:, m, start : start + BANK],
+                    scalar1=THIRD,
+                    scalar2=0.0,
+                    op0=ALU.mult,
+                    op1=ALU.add,
+                )
+
+        load_operands(*rounds[0])
+        for r in range(len(rounds)):
+            if r + 1 < len(rounds):
+                load_operands(*rounds[r + 1])
+            load_residual(*rounds[r])
+            third_of_residual(*rounds[r])
+
+        grouped_of = {}
+
+        def regroup(bank, i):
+            grouped = stage.tile([P, BANK, PACK], BF16, align_bytes=64)
+            grouped_of[(bank, i)] = grouped
+            half = BANK // 2
+            first, end = load_span(bank)
+            raw = raw_of[(i, first)]
+            start = bank * BANK - first
+            nc.vector.tensor_copy(
+                out=grouped[:, :half, :].rearrange("p (c r) t -> p c t r", r=4),
+                in_=raw[:, :, start : start + half].rearrange("p t (c r) -> p c t r", r=4),
+            )
+            nc.scalar.copy(
+                out=grouped[:, half:, :].rearrange("p (c r) t -> p c t r", r=4),
+                in_=raw[:, :, start + half : start + BANK].rearrange("p t (c r) -> p c t r", r=4),
+            )
+
+        def quantise(bank, i):
+            cols = slice(bank * BANK, (bank + 1) * BANK)
+            positive = grouped_of[(bank, i)][:].rearrange("p w t -> p (w t)")
+            signed = [(plus(i), positive)]
+            if i > 0:
+                negated = stage.tile([P, BANK * PACK], BF16, align_bytes=64)
+                nc.vector.tensor_scalar_mul(out=negated[:], in0=positive, scalar1=-1.0)
+                signed.append((minus(i), negated[:]))
+            for v, values in signed:
+                nc.vector.quantize_mx(
+                    out=f_codes[:, v, cols].bitcast(FP8X4),
+                    scales=f_scales[:, v, cols],
+                    in_=values,
+                )
+
+        def two_passes(acc, m, cols, terms):
+            rows = slice(m * P, (m + 1) * P)
+            for n, (e, v) in enumerate(terms):
+                nc.tensor.matmul_mx(
+                    out=acc[:],
+                    lhsT=r_codes[:, e, rows].bitcast(FP8X4),
+                    lhsT_scale=r_scales[:, e, rows],
+                    rhs=f_codes[:, v, cols].bitcast(FP8X4),
+                    rhs_scale=f_scales[:, v, cols],
+                    start=(n == 0),
+                    stop=(n == len(terms) - 1),
+                )
+
+        def output_tile(r, m):
+            bank, left_out = rounds[r]
+            i, j = others(left_out)
+            cols = slice(bank * BANK, (bank + 1) * BANK)
+
+            dif = psum.tile([P, BANK], F32)
+            two_passes(dif, m, cols, ((group(i, j), plus(i)), (group(j, i), minus(j))))
+            squares = stage.tile([P, BANK], BF16)
+            nc.scalar.activation(
+                out=squares[:],
+                in_=dif[:],
+                func=ACT.Square,
+                accum_out=square_sums[:, r * ROW_TILES + m : r * ROW_TILES + m + 1],
+            )
+
+            agg = psum.tile([P, BANK], F32)
+            two_passes(agg, m, cols, ((group(i, left_out), plus(i)), (group(j, left_out), plus(j))))
+            nc.vector.scalar_tensor_tensor(
+                out=result[:, left_out, m, cols],
+                in0=agg[:],
+                scalar=THIRD,
+                in1=result[:, left_out, m, cols],
+                op0=ALU.mult,
+                op1=ALU.add,
+            )
+            nc.sync.dma_start(
+                out=out_0[left_out, m * P : (m + 1) * P, cols], in_=result[:, left_out, m, cols]
+            )
+
+        regroup(*steps[0])
+        regroup(*steps[1])
+        quantise(*steps[0])
+        quantise(*steps[1])
+        regroup(*steps[2])
+        quantise(*steps[2])
+        for r in range(len(rounds)):
+            ahead = steps[r + 2] if 1 <= r and r + 2 < len(steps) else None
+            output_tile(r, 0)
+            if ahead:
+                regroup(*ahead)
+            output_tile(r, 1)
+            if ahead:
+                quantise(*ahead)
+            output_tile(r, 2)
+            output_tile(r, 3)
+
+        total = psum.tile([P, BANK], F32, tag="dif")
+        n_sums = len(rounds) * ROW_TILES
+        nc.tensor.matmul(out=total[:, :n_sums], lhsT=ones[:], rhs=square_sums[:], start=True, stop=True)
+        nc.vector.tensor_reduce(
+            out=loss_sum[:], in_=total[:, :n_sums], axis=mybir.AxisListType.X, op=ALU.add
+        )
+        nc.vector.tensor_scalar_mul(out=loss[:], in0=loss_sum[:], scalar1=LOSS_WEIGHT)
+        loss_out = out_1
+        for axis in range(2 - out_1.ndim):
+            loss_out = loss_out.unsqueeze(0)
+        nc.sync.dma_start(out=loss_out, in_=loss[0:1, 0:1])

@@ -25,6 +25,8 @@ SCALE_ROWS = FEATURES // 32
 THIRD = 1.0 / 3.0
 LOSS_WEIGHT = 0.1 * 0.5 * 2.0
 
+GPSIMD_ROW_TILES = 3
+
 LOAD_SPANS = ((0, 1), (1, BANKS))
 
 FLOPS = 2 * FEATURES * FEATURES * COLUMNS * 2 * PATCHES * (PATCHES - 1)
@@ -82,7 +84,7 @@ def tile_sheaflayer_t_e_kernel(tc, F, R_words, R_scales, out_0, out_1):
                 resid_of[(i, first)] = keep.tile(
                     [P, ROW_TILES, width], BF16, name="resid_%d_%d" % (i, first)
                 )
-        result = keep.tile([P, PATCHES, ROW_TILES, COLUMNS], F32)
+        result = keep.tile([P, PATCHES, BANKS, ROW_TILES, BANK], F32)
         f_codes = keep.tile([P, VERSIONS, COLUMNS], U32, align_bytes=64)
         f_scales = keep.tile([P, VERSIONS, COLUMNS], U8, align_bytes=64)
         r_codes = keep.tile([P, GROUPS, FEATURES], U32, align_bytes=64)
@@ -138,26 +140,36 @@ def tile_sheaflayer_t_e_kernel(tc, F, R_words, R_scales, out_0, out_1):
                 F[left_out, :, first:end].rearrange("(m p) b -> p m b", p=P),
             )
 
-        def third_of_residual(bank, left_out):
-            cols = slice(bank * BANK, (bank + 1) * BANK)
+        def residual_rows(bank, left_out, rows):
             first, end = load_span(bank)
             start = bank * BANK - first
-            for m in range(ROW_TILES):
-                nc.gpsimd.tensor_scalar(
-                    out=result[:, left_out, m, cols],
-                    in0=resid_of[(left_out, first)][:, m, start : start + BANK],
-                    scalar1=THIRD,
-                    scalar2=0.0,
-                    op0=ALU.mult,
-                    op1=ALU.add,
-                )
+            return resid_of[(left_out, first)][:, rows, start : start + BANK]
+
+        def third_on_gpsimd(bank, left_out):
+            rows = slice(0, GPSIMD_ROW_TILES)
+            nc.gpsimd.tensor_scalar(
+                out=result[:, left_out, bank, rows, :],
+                in0=residual_rows(bank, left_out, rows),
+                scalar1=THIRD,
+                scalar2=0.0,
+                op0=ALU.mult,
+                op1=ALU.add,
+            )
+
+        def third_on_scalar(bank, left_out):
+            rows = slice(GPSIMD_ROW_TILES, ROW_TILES)
+            nc.scalar.mul(
+                out=result[:, left_out, bank, rows, :],
+                in_=residual_rows(bank, left_out, rows),
+                mul=THIRD,
+            )
 
         load_operands(*rounds[0])
         for r in range(len(rounds)):
             if r + 1 < len(rounds):
                 load_operands(*rounds[r + 1])
             load_residual(*rounds[r])
-            third_of_residual(*rounds[r])
+            third_on_gpsimd(*rounds[r])
 
         grouped_of = {}
 
@@ -223,15 +235,15 @@ def tile_sheaflayer_t_e_kernel(tc, F, R_words, R_scales, out_0, out_1):
             agg = psum.tile([P, BANK], F32)
             two_passes(agg, m, cols, ((group(i, left_out), plus(i)), (group(j, left_out), plus(j))))
             nc.vector.scalar_tensor_tensor(
-                out=result[:, left_out, m, cols],
+                out=result[:, left_out, bank, m, :],
                 in0=agg[:],
                 scalar=THIRD,
-                in1=result[:, left_out, m, cols],
+                in1=result[:, left_out, bank, m, :],
                 op0=ALU.mult,
                 op1=ALU.add,
             )
             nc.sync.dma_start(
-                out=out_0[left_out, m * P : (m + 1) * P, cols], in_=result[:, left_out, m, cols]
+                out=out_0[left_out, m * P : (m + 1) * P, cols], in_=result[:, left_out, bank, m, :]
             )
 
         regroup(*steps[0])
@@ -249,6 +261,7 @@ def tile_sheaflayer_t_e_kernel(tc, F, R_words, R_scales, out_0, out_1):
             if ahead:
                 quantise(*ahead)
             output_tile(r, 2)
+            third_on_scalar(*rounds[r])
             output_tile(r, 3)
 
         total = psum.tile([P, BANK], F32, tag="dif")

@@ -25,9 +25,7 @@ SCALE_ROWS = FEATURES // 32
 THIRD = 1.0 / 3.0
 LOSS_WEIGHT = 0.1 * 0.5 * 2.0
 
-GPSIMD_ROW_TILES = 3
-
-LOAD_SPANS = ((0, 1), (1, BANKS))
+LOAD_SPANS = ((0, 1), (1, 2), (2, 3))
 
 FLOPS = 2 * FEATURES * FEATURES * COLUMNS * 2 * PATCHES * (PATCHES - 1)
 BYTES = (
@@ -84,7 +82,7 @@ def tile_sheaflayer_t_e_kernel(tc, F, R_words, R_scales, out_0, out_1):
                 resid_of[(i, first)] = keep.tile(
                     [P, ROW_TILES, width], BF16, name="resid_%d_%d" % (i, first)
                 )
-        result = keep.tile([P, PATCHES, BANKS, ROW_TILES, BANK], F32)
+        result = keep.tile([P, PATCHES, ROW_TILES, COLUMNS], F32)
         f_codes = keep.tile([P, VERSIONS, COLUMNS], U32, align_bytes=64)
         f_scales = keep.tile([P, VERSIONS, COLUMNS], U8, align_bytes=64)
         r_codes = keep.tile([P, GROUPS, FEATURES], U32, align_bytes=64)
@@ -140,36 +138,26 @@ def tile_sheaflayer_t_e_kernel(tc, F, R_words, R_scales, out_0, out_1):
                 F[left_out, :, first:end].rearrange("(m p) b -> p m b", p=P),
             )
 
-        def residual_rows(bank, left_out, rows):
+        def third_of_residual(bank, left_out):
+            cols = slice(bank * BANK, (bank + 1) * BANK)
             first, end = load_span(bank)
             start = bank * BANK - first
-            return resid_of[(left_out, first)][:, rows, start : start + BANK]
-
-        def third_on_gpsimd(bank, left_out):
-            rows = slice(0, GPSIMD_ROW_TILES)
-            nc.gpsimd.tensor_scalar(
-                out=result[:, left_out, bank, rows, :],
-                in0=residual_rows(bank, left_out, rows),
-                scalar1=THIRD,
-                scalar2=0.0,
-                op0=ALU.mult,
-                op1=ALU.add,
-            )
-
-        def third_on_scalar(bank, left_out):
-            rows = slice(GPSIMD_ROW_TILES, ROW_TILES)
-            nc.scalar.mul(
-                out=result[:, left_out, bank, rows, :],
-                in_=residual_rows(bank, left_out, rows),
-                mul=THIRD,
-            )
+            for m in range(ROW_TILES):
+                nc.gpsimd.tensor_scalar(
+                    out=result[:, left_out, m, cols],
+                    in0=resid_of[(left_out, first)][:, m, start : start + BANK],
+                    scalar1=THIRD,
+                    scalar2=0.0,
+                    op0=ALU.mult,
+                    op1=ALU.add,
+                )
 
         load_operands(*rounds[0])
         for r in range(len(rounds)):
             if r + 1 < len(rounds):
                 load_operands(*rounds[r + 1])
             load_residual(*rounds[r])
-            third_on_gpsimd(*rounds[r])
+            third_of_residual(*rounds[r])
 
         grouped_of = {}
 
@@ -235,15 +223,15 @@ def tile_sheaflayer_t_e_kernel(tc, F, R_words, R_scales, out_0, out_1):
             agg = psum.tile([P, BANK], F32)
             two_passes(agg, m, cols, ((group(i, left_out), plus(i)), (group(j, left_out), plus(j))))
             nc.vector.scalar_tensor_tensor(
-                out=result[:, left_out, bank, m, :],
+                out=result[:, left_out, m, cols],
                 in0=agg[:],
                 scalar=THIRD,
-                in1=result[:, left_out, bank, m, :],
+                in1=result[:, left_out, m, cols],
                 op0=ALU.mult,
                 op1=ALU.add,
             )
             nc.sync.dma_start(
-                out=out_0[left_out, m * P : (m + 1) * P, cols], in_=result[:, left_out, bank, m, :]
+                out=out_0[left_out, m * P : (m + 1) * P, cols], in_=result[:, left_out, m, cols]
             )
 
         regroup(*steps[0])
@@ -253,15 +241,14 @@ def tile_sheaflayer_t_e_kernel(tc, F, R_words, R_scales, out_0, out_1):
         regroup(*steps[2])
         quantise(*steps[2])
         for r in range(len(rounds)):
-            ahead = steps[r + 2] if 1 <= r and r + 2 < len(steps) else None
+            ahead = steps[r + 3] if r + 3 < len(steps) else None
             output_tile(r, 0)
-            if ahead:
-                regroup(*ahead)
             output_tile(r, 1)
             if ahead:
-                quantise(*ahead)
+                regroup(*ahead)
             output_tile(r, 2)
-            third_on_scalar(*rounds[r])
+            if ahead:
+                quantise(*ahead)
             output_tile(r, 3)
 
         total = psum.tile([P, BANK], F32, tag="dif")

@@ -25,7 +25,9 @@ SCALE_ROWS = FEATURES // 32
 THIRD = 1.0 / 3.0
 LOSS_WEIGHT = 0.1 * 0.5 * 2.0
 
-LOAD_SPANS = ((0, 1), (1, 2), (2, 3))
+RAW_SPANS = ((0, 1), (1, 2), (2, 3))
+RESID_SPANS = ((0, 1), (1, 3))
+STORE_SPANS = ((0, 2), (2, 3))
 
 FLOPS = 2 * FEATURES * FEATURES * COLUMNS * 2 * PATCHES * (PATCHES - 1)
 BYTES = (
@@ -54,8 +56,8 @@ def others(left_out):
     return [i for i in range(PATCHES) if i != left_out]
 
 
-def load_span(bank):
-    for first, end in LOAD_SPANS:
+def span_of(bank, spans):
+    for first, end in spans:
         if first <= bank < end:
             return first * BANK, end * BANK
     raise ValueError(bank)
@@ -76,12 +78,17 @@ def tile_sheaflayer_t_e_kernel(tc, F, R_words, R_scales, out_0, out_1):
         raw_of = {}
         resid_of = {}
         for i in range(PATCHES):
-            for first_bank, end_bank in LOAD_SPANS:
-                first, width = first_bank * BANK, (end_bank - first_bank) * BANK
-                raw_of[(i, first)] = keep.tile([P, PACK, width], BF16, name="raw_%d_%d" % (i, first))
-                resid_of[(i, first)] = keep.tile(
-                    [P, ROW_TILES, width], BF16, name="resid_%d_%d" % (i, first)
-                )
+            for bank in range(BANKS):
+                first, end = span_of(bank, RAW_SPANS)
+                if first == bank * BANK:
+                    raw_of[(i, first)] = keep.tile(
+                        [P, PACK, end - first], BF16, name="raw_%d_%d" % (i, first)
+                    )
+                first, end = span_of(bank, RESID_SPANS)
+                if first == bank * BANK:
+                    resid_of[(i, first)] = keep.tile(
+                        [P, ROW_TILES, end - first], BF16, name="resid_%d_%d" % (i, first)
+                    )
         result = keep.tile([P, PATCHES, ROW_TILES, COLUMNS], F32)
         f_codes = keep.tile([P, VERSIONS, COLUMNS], U32, align_bytes=64)
         f_scales = keep.tile([P, VERSIONS, COLUMNS], U8, align_bytes=64)
@@ -103,7 +110,7 @@ def tile_sheaflayer_t_e_kernel(tc, F, R_words, R_scales, out_0, out_1):
                 nc.sync.dma_start(out=out, in_=in_)
 
         def load_raw(bank, i):
-            first, end = load_span(bank)
+            first, end = span_of(bank, RAW_SPANS)
             load_once(
                 ("raw", i, first),
                 raw_of[(i, first)][:],
@@ -131,7 +138,7 @@ def tile_sheaflayer_t_e_kernel(tc, F, R_words, R_scales, out_0, out_1):
                 load_weights(e)
 
         def load_residual(bank, left_out):
-            first, end = load_span(bank)
+            first, end = span_of(bank, RESID_SPANS)
             load_once(
                 ("resid", left_out, first),
                 resid_of[(left_out, first)][:],
@@ -140,7 +147,7 @@ def tile_sheaflayer_t_e_kernel(tc, F, R_words, R_scales, out_0, out_1):
 
         def third_of_residual(bank, left_out):
             cols = slice(bank * BANK, (bank + 1) * BANK)
-            first, end = load_span(bank)
+            first, end = span_of(bank, RESID_SPANS)
             start = bank * BANK - first
             for m in range(ROW_TILES):
                 nc.gpsimd.tensor_scalar(
@@ -165,7 +172,7 @@ def tile_sheaflayer_t_e_kernel(tc, F, R_words, R_scales, out_0, out_1):
             grouped = stage.tile([P, BANK, PACK], BF16, align_bytes=64)
             grouped_of[(bank, i)] = grouped
             half = BANK // 2
-            first, end = load_span(bank)
+            first, end = span_of(bank, RAW_SPANS)
             raw = raw_of[(i, first)]
             start = bank * BANK - first
             nc.vector.tensor_copy(
@@ -230,9 +237,12 @@ def tile_sheaflayer_t_e_kernel(tc, F, R_words, R_scales, out_0, out_1):
                 op0=ALU.mult,
                 op1=ALU.add,
             )
-            nc.sync.dma_start(
-                out=out_0[left_out, m * P : (m + 1) * P, cols], in_=result[:, left_out, m, cols]
-            )
+            first, end = span_of(bank, STORE_SPANS)
+            if (bank + 1) * BANK == end:
+                nc.sync.dma_start(
+                    out=out_0[left_out, m * P : (m + 1) * P, first:end],
+                    in_=result[:, left_out, m, first:end],
+                )
 
         regroup(*steps[0])
         regroup(*steps[1])
@@ -244,12 +254,12 @@ def tile_sheaflayer_t_e_kernel(tc, F, R_words, R_scales, out_0, out_1):
             ahead = steps[r + 3] if r + 3 < len(steps) else None
             output_tile(r, 0)
             output_tile(r, 1)
-            if ahead:
-                regroup(*ahead)
             output_tile(r, 2)
             if ahead:
-                quantise(*ahead)
+                regroup(*ahead)
             output_tile(r, 3)
+            if ahead:
+                quantise(*ahead)
 
         total = psum.tile([P, BANK], F32, tag="dif")
         n_sums = len(rounds) * ROW_TILES

@@ -21,6 +21,7 @@ ROW_TILES = FEATURES // P
 BANKS = COLUMNS // BANK
 GROUPS = 8
 SCALE_ROWS = FEATURES // 32
+R_PAD_WORDS = 48
 
 THIRD = 1.0 / 3.0
 LOSS_WEIGHT = 0.1 * 0.5 * 2.0
@@ -90,10 +91,11 @@ def tile_sheaflayer_t_e_kernel(tc, F, R_words, R_scales, out_0, out_1):
                         [P, ROW_TILES, end - first], BF16, name="resid_%d_%d" % (i, first)
                     )
         result = keep.tile([P, PATCHES, ROW_TILES, COLUMNS], F32)
-        f_codes = keep.tile([P, VERSIONS, COLUMNS], U32, align_bytes=64)
-        f_scales = keep.tile([P, VERSIONS, COLUMNS], U8, align_bytes=64)
-        r_codes = keep.tile([P, GROUPS, FEATURES], U32, align_bytes=64)
-        r_scales = keep.tile([P, GROUPS, FEATURES], U8, align_bytes=64)
+        f_codes = keep.tile([P, VERSIONS, COLUMNS], U32, align_bytes=256)
+        f_scales = keep.tile([P, VERSIONS, COLUMNS], U8, align_bytes=256)
+        r_codes_padded = keep.tile([P, R_PAD_WORDS + GROUPS * FEATURES], U32, align_bytes=256)
+        r_codes = r_codes_padded[:, R_PAD_WORDS:].rearrange("p (g n) -> p g n", g=GROUPS)
+        r_scales = keep.tile([P, GROUPS, FEATURES], U8, align_bytes=256)
         ones = keep.tile([P, P], F32)
         square_sums = keep.tile([P, len(rounds) * ROW_TILES], F32)
         loss_sum = keep.tile([P, 1], F32)

@@ -19,15 +19,15 @@ PACK = 4
 BANK = 512
 ROW_TILES = FEATURES // P
 BANKS = COLUMNS // BANK
-GROUPS = 8
 SCALE_ROWS = FEATURES // 32
+PLANES = 4
+PLANE_TILES = 2
 R_PAD_WORDS = 48
 
 THIRD = 1.0 / 3.0
 LOSS_WEIGHT = 0.1 * 0.5 * 2.0
 
 RAW_SPANS = ((0, 1), (1, 2), (2, 3))
-RESID_SPANS = ((0, 1), (1, 3))
 STORE_SPANS = ((0, 2), (2, 3))
 
 FLOPS = 2 * FEATURES * FEATURES * COLUMNS * 2 * PATCHES * (PATCHES - 1)
@@ -66,6 +66,7 @@ def span_of(bank, spans):
 
 def tile_sheaflayer_t_e_kernel(tc, F, R_words, R_scales, out_0, out_1):
     nc = tc.nc
+    used_groups = [group(i, j) for i in range(PATCHES) for j in range(PATCHES) if i != j]
 
     rounds = [(bank, left_out) for bank in range(BANKS) for left_out in (2, 1, 0)]
     steps = [(bank, i) for bank in range(BANKS) for i in range(PATCHES)]
@@ -77,7 +78,6 @@ def tile_sheaflayer_t_e_kernel(tc, F, R_words, R_scales, out_0, out_1):
         ctx.enter_context(tc.manual_schedule())
 
         raw_of = {}
-        resid_of = {}
         for i in range(PATCHES):
             for bank in range(BANKS):
                 first, end = span_of(bank, RAW_SPANS)
@@ -85,17 +85,16 @@ def tile_sheaflayer_t_e_kernel(tc, F, R_words, R_scales, out_0, out_1):
                     raw_of[(i, first)] = keep.tile(
                         [P, PACK, end - first], BF16, name="raw_%d_%d" % (i, first)
                     )
-                first, end = span_of(bank, RESID_SPANS)
-                if first == bank * BANK:
-                    resid_of[(i, first)] = keep.tile(
-                        [P, ROW_TILES, end - first], BF16, name="resid_%d_%d" % (i, first)
-                    )
         result = keep.tile([P, PATCHES, ROW_TILES, COLUMNS], F32)
         f_codes = keep.tile([P, VERSIONS, COLUMNS], U32, align_bytes=256)
         f_scales = keep.tile([P, VERSIONS, COLUMNS], U8, align_bytes=256)
-        r_codes_padded = keep.tile([P, R_PAD_WORDS + GROUPS * FEATURES], U32, align_bytes=256)
-        r_codes = r_codes_padded[:, R_PAD_WORDS:].rearrange("p (g n) -> p g n", g=GROUPS)
-        r_scales = keep.tile([P, GROUPS, FEATURES], U8, align_bytes=256)
+        n_used = len(used_groups)
+        r_codes_padded = keep.tile([P, R_PAD_WORDS + n_used * FEATURES], U32, align_bytes=256)
+        r_codes = r_codes_padded[:, R_PAD_WORDS:].rearrange("p (g n) -> p g n", g=n_used)
+        r_scales = keep.tile([P, PLANE_TILES, FEATURES], U8, align_bytes=256)
+        w_codes_padded = keep.tile([P, R_PAD_WORDS + n_used * FEATURES], U32, align_bytes=256)
+        w_codes = w_codes_padded[:, R_PAD_WORDS:].rearrange("p (g n) -> p g n", g=n_used)
+        w_scales = keep.tile([P, PLANE_TILES, FEATURES], U8, align_bytes=256)
         ones = keep.tile([P, P], F32)
         square_sums = keep.tile([P, len(rounds) * ROW_TILES], F32)
         loss_sum = keep.tile([P, 1], F32)
@@ -120,15 +119,18 @@ def tile_sheaflayer_t_e_kernel(tc, F, R_words, R_scales, out_0, out_1):
             )
 
         def load_weights(e):
-            for r in range(4):
+            h = e // PLANES
+            for quadrant in range(4):
                 load_once(
-                    ("scales", r),
-                    r_scales[r:P:32, :, :].bitcast(I32),
-                    R_scales[0:GROUPS, r:SCALE_ROWS:4, :].rearrange("g q n -> q g n").bitcast(I32),
+                    ("scales", h, quadrant),
+                    r_scales[32 * quadrant : 32 * quadrant + 4 * PLANES, h, :].bitcast(I32),
+                    R_scales[
+                        PLANES * h : PLANES * (h + 1), 4 * quadrant : 4 * quadrant + 4, :
+                    ].bitcast(I32),
                 )
             load_once(
                 ("codes", e),
-                r_codes[:, e, :].bitcast(I32),
+                r_codes[:, used_groups.index(e), :].bitcast(I32),
                 R_words[e].rearrange("p n t -> p (n t)").bitcast(I32),
             )
 
@@ -139,22 +141,14 @@ def tile_sheaflayer_t_e_kernel(tc, F, R_words, R_scales, out_0, out_1):
             for e in (group(i, j), group(j, i), group(i, left_out), group(j, left_out)):
                 load_weights(e)
 
-        def load_residual(bank, left_out):
-            first, end = span_of(bank, RESID_SPANS)
-            load_once(
-                ("resid", left_out, first),
-                resid_of[(left_out, first)][:],
-                F[left_out, :, first:end].rearrange("(m p) b -> p m b", p=P),
-            )
-
         def third_of_residual(bank, left_out):
             cols = slice(bank * BANK, (bank + 1) * BANK)
-            first, end = span_of(bank, RESID_SPANS)
+            first, end = span_of(bank, RAW_SPANS)
             start = bank * BANK - first
             for m in range(ROW_TILES):
                 nc.gpsimd.tensor_scalar(
                     out=result[:, left_out, m, cols],
-                    in0=resid_of[(left_out, first)][:, m, start : start + BANK],
+                    in0=raw_of[(left_out, first)][:, m, start : start + BANK],
                     scalar1=THIRD,
                     scalar2=0.0,
                     op0=ALU.mult,
@@ -165,7 +159,7 @@ def tile_sheaflayer_t_e_kernel(tc, F, R_words, R_scales, out_0, out_1):
         for r in range(len(rounds)):
             if r + 1 < len(rounds):
                 load_operands(*rounds[r + 1])
-            load_residual(*rounds[r])
+            load_raw(*rounds[r])
             third_of_residual(*rounds[r])
 
         grouped_of = {}
@@ -201,26 +195,42 @@ def tile_sheaflayer_t_e_kernel(tc, F, R_words, R_scales, out_0, out_1):
                     in_=values,
                 )
 
-        def two_passes(acc, m, cols, terms):
+        def permute_scales():
+            for t in range(PACK):
+                nc.vector.tensor_copy(
+                    out=w_scales[:, :, t * P : (t + 1) * P],
+                    in_=r_scales[:, :, t:FEATURES:PACK],
+                )
+
+        def permute_codes(e):
+            g = used_groups.index(e)
+            nc.vector.tensor_copy(
+                out=w_codes[:, g, :].bitcast(I32).rearrange("p (t m) -> p t m", t=PACK),
+                in_=r_codes[:, g, :].bitcast(I32).rearrange("p (m t) -> p t m", t=PACK),
+            )
+
+        def two_passes(acc, m, cols, terms, codes, scales):
             rows = slice(m * P, (m + 1) * P)
             for n, (e, v) in enumerate(terms):
                 nc.tensor.matmul_mx(
                     out=acc[:],
-                    lhsT=r_codes[:, e, rows].bitcast(FP8X4),
-                    lhsT_scale=r_scales[:, e, rows],
+                    lhsT=codes[:, used_groups.index(e), rows].bitcast(FP8X4),
+                    lhsT_scale=scales[4 * (e % PLANES) : P, e // PLANES, rows],
                     rhs=f_codes[:, v, cols].bitcast(FP8X4),
                     rhs_scale=f_scales[:, v, cols],
                     start=(n == 0),
                     stop=(n == len(terms) - 1),
                 )
 
-        def output_tile(r, m):
+        def dif_tile(r, m):
             bank, left_out = rounds[r]
             i, j = others(left_out)
             cols = slice(bank * BANK, (bank + 1) * BANK)
 
             dif = psum.tile([P, BANK], F32)
-            two_passes(dif, m, cols, ((group(i, j), plus(i)), (group(j, i), minus(j))))
+            two_passes(
+                dif, m, cols, ((group(i, j), plus(i)), (group(j, i), minus(j))), r_codes, r_scales
+            )
             squares = stage.tile([P, BANK], BF16)
             nc.scalar.activation(
                 out=squares[:],
@@ -229,8 +239,20 @@ def tile_sheaflayer_t_e_kernel(tc, F, R_words, R_scales, out_0, out_1):
                 accum_out=square_sums[:, r * ROW_TILES + m : r * ROW_TILES + m + 1],
             )
 
+        def agg_tile(r, m):
+            bank, left_out = rounds[r]
+            i, j = others(left_out)
+            cols = slice(bank * BANK, (bank + 1) * BANK)
+
             agg = psum.tile([P, BANK], F32)
-            two_passes(agg, m, cols, ((group(i, left_out), plus(i)), (group(j, left_out), plus(j))))
+            two_passes(
+                agg,
+                m,
+                cols,
+                ((group(i, left_out), plus(i)), (group(j, left_out), plus(j))),
+                w_codes,
+                w_scales,
+            )
             nc.vector.scalar_tensor_tensor(
                 out=result[:, left_out, m, cols],
                 in0=agg[:],
@@ -242,24 +264,46 @@ def tile_sheaflayer_t_e_kernel(tc, F, R_words, R_scales, out_0, out_1):
             first, end = span_of(bank, STORE_SPANS)
             if (bank + 1) * BANK == end:
                 nc.sync.dma_start(
-                    out=out_0[left_out, m * P : (m + 1) * P, first:end],
+                    out=out_0[left_out].rearrange("(p t) b -> p t b", t=PACK)[:, m, first:end],
                     in_=result[:, left_out, m, first:end],
                 )
+
+        def output_tile(r, m):
+            dif_tile(r, m)
+            agg_tile(r, m)
+
+        def permute_for(r):
+            bank, left_out = rounds[r]
+            for i in others(left_out):
+                permute_codes(group(i, left_out))
 
         regroup(*steps[0])
         regroup(*steps[1])
         quantise(*steps[0])
         quantise(*steps[1])
+        permute_scales()
+        permute_for(0)
         regroup(*steps[2])
         quantise(*steps[2])
         for r in range(len(rounds)):
             ahead = steps[r + 3] if r + 3 < len(steps) else None
-            output_tile(r, 0)
-            output_tile(r, 1)
-            output_tile(r, 2)
+            if r == 0:
+                for m in range(ROW_TILES):
+                    dif_tile(r, m)
+                for m in range(ROW_TILES - 1):
+                    agg_tile(r, m)
+            else:
+                output_tile(r, 0)
+                output_tile(r, 1)
+                output_tile(r, 2)
+            if r + 1 < PATCHES:
+                permute_for(r + 1)
             if ahead:
                 regroup(*ahead)
-            output_tile(r, 3)
+            if r == 0:
+                agg_tile(r, 3)
+            else:
+                output_tile(r, 3)
             if ahead:
                 quantise(*ahead)
 

@@ -24,6 +24,10 @@ PLANES = 4
 PLANE_TILES = 2
 R_PAD_WORDS = 48
 
+VECTOR_COLUMNS_HEAD = 320
+VECTOR_COLUMNS = 256
+SCALERS = "gggs"
+
 THIRD = 1.0 / 3.0
 LOSS_WEIGHT = 0.1 * 0.5 * 2.0
 
@@ -97,7 +101,7 @@ def tile_sheaflayer_t_e_kernel(tc, F, R_words, R_scales, out_0, out_1):
         w_scales = keep.tile([P, PLANE_TILES, FEATURES], U8, align_bytes=256)
         ones = keep.tile([P, P], F32)
         square_sums = keep.tile([P, len(rounds) * ROW_TILES], F32)
-        loss_sum = keep.tile([P, 1], F32)
+        weighted = keep.tile([P, len(rounds) * ROW_TILES], F32)
         loss = keep.tile([P, 1], F32)
 
         nc.vector.memset(r_scales[:].bitcast(I32), 0)
@@ -134,40 +138,25 @@ def tile_sheaflayer_t_e_kernel(tc, F, R_words, R_scales, out_0, out_1):
                 R_words[e].rearrange("p n t -> p (n t)").bitcast(I32),
             )
 
-        def load_operands(bank, left_out):
-            i, j = others(left_out)
+        load_raw(0, 0)
+        load_raw(0, 1)
+        load_weights(group(0, 1))
+        load_weights(group(1, 0))
+        load_raw(0, 2)
+        load_weights(group(0, 2))
+        load_weights(group(1, 2))
+        load_raw(1, 0)
+        load_weights(group(2, 0))
+        load_weights(group(2, 1))
+        for bank, i in steps:
             load_raw(bank, i)
-            load_raw(bank, j)
-            for e in (group(i, j), group(j, i), group(i, left_out), group(j, left_out)):
-                load_weights(e)
-
-        def third_of_residual(bank, left_out):
-            cols = slice(bank * BANK, (bank + 1) * BANK)
-            first, end = span_of(bank, RAW_SPANS)
-            start = bank * BANK - first
-            for m in range(ROW_TILES):
-                nc.gpsimd.tensor_scalar(
-                    out=result[:, left_out, m, cols],
-                    in0=raw_of[(left_out, first)][:, m, start : start + BANK],
-                    scalar1=THIRD,
-                    scalar2=0.0,
-                    op0=ALU.mult,
-                    op1=ALU.add,
-                )
-
-        load_operands(*rounds[0])
-        for r in range(len(rounds)):
-            if r + 1 < len(rounds):
-                load_operands(*rounds[r + 1])
-            load_raw(*rounds[r])
-            third_of_residual(*rounds[r])
 
         grouped_of = {}
 
         def regroup(bank, i):
             grouped = stage.tile([P, BANK, PACK], BF16, align_bytes=64)
             grouped_of[(bank, i)] = grouped
-            half = BANK // 2
+            half = VECTOR_COLUMNS_HEAD if bank == 0 else VECTOR_COLUMNS
             first, end = span_of(bank, RAW_SPANS)
             raw = raw_of[(i, first)]
             start = bank * BANK - first
@@ -187,7 +176,7 @@ def tile_sheaflayer_t_e_kernel(tc, F, R_words, R_scales, out_0, out_1):
             if i > 0:
                 negated = stage.tile([P, BANK * PACK], BF16, align_bytes=64)
                 nc.vector.tensor_scalar_mul(out=negated[:], in0=positive, scalar1=-1.0)
-                signed.append((minus(i), negated[:]))
+                signed = [(minus(i), negated[:]), (plus(i), positive)]
             for v, values in signed:
                 nc.vector.quantize_mx(
                     out=f_codes[:, v, cols].bitcast(FP8X4),
@@ -202,9 +191,9 @@ def tile_sheaflayer_t_e_kernel(tc, F, R_words, R_scales, out_0, out_1):
                     in_=r_scales[:, :, t:FEATURES:PACK],
                 )
 
-        def permute_codes(e):
+        def permute_codes(e, engine):
             g = used_groups.index(e)
-            nc.vector.tensor_copy(
+            engine.tensor_copy(
                 out=w_codes[:, g, :].bitcast(I32).rearrange("p (t m) -> p t m", t=PACK),
                 in_=r_codes[:, g, :].bitcast(I32).rearrange("p (m t) -> p t m", t=PACK),
             )
@@ -253,14 +242,25 @@ def tile_sheaflayer_t_e_kernel(tc, F, R_words, R_scales, out_0, out_1):
                 w_codes,
                 w_scales,
             )
-            nc.vector.scalar_tensor_tensor(
+            first, end = span_of(bank, RAW_SPANS)
+            start = bank * BANK - first
+            nc.vector.tensor_tensor(
                 out=result[:, left_out, m, cols],
                 in0=agg[:],
-                scalar=THIRD,
-                in1=result[:, left_out, m, cols],
-                op0=ALU.mult,
-                op1=ALU.add,
+                in1=raw_of[(left_out, first)][:, m, start : start + BANK],
+                op=ALU.add,
             )
+            if SCALERS[m] == "g":
+                nc.gpsimd.tensor_scalar(
+                    out=result[:, left_out, m, cols],
+                    in0=result[:, left_out, m, cols],
+                    scalar1=THIRD,
+                    scalar2=0.0,
+                    op0=ALU.mult,
+                    op1=ALU.add,
+                )
+            else:
+                nc.scalar.mul(result[:, left_out, m, cols], result[:, left_out, m, cols], THIRD)
             first, end = span_of(bank, STORE_SPANS)
             if (bank + 1) * BANK == end:
                 nc.sync.dma_start(
@@ -268,52 +268,46 @@ def tile_sheaflayer_t_e_kernel(tc, F, R_words, R_scales, out_0, out_1):
                     in_=result[:, left_out, m, first:end],
                 )
 
-        def output_tile(r, m):
-            dif_tile(r, m)
-            agg_tile(r, m)
-
-        def permute_for(r):
+        def permute_for(r, engine):
             bank, left_out = rounds[r]
             for i in others(left_out):
-                permute_codes(group(i, left_out))
+                permute_codes(group(i, left_out), engine)
 
         regroup(*steps[0])
         regroup(*steps[1])
         quantise(*steps[0])
         quantise(*steps[1])
         permute_scales()
-        permute_for(0)
+        permute_for(0, nc.vector)
         regroup(*steps[2])
-        quantise(*steps[2])
+        permute_for(1, nc.gpsimd)
+        permute_for(2, nc.gpsimd)
         for r in range(len(rounds)):
-            ahead = steps[r + 3] if r + 3 < len(steps) else None
-            if r == 0:
+            if r + 2 < len(steps):
+                quantise(*steps[r + 2])
+            if r == len(rounds) - 1:
                 for m in range(ROW_TILES):
-                    dif_tile(r, m)
-                for m in range(ROW_TILES - 1):
                     agg_tile(r, m)
-            else:
-                output_tile(r, 0)
-                output_tile(r, 1)
-                output_tile(r, 2)
-            if r + 1 < PATCHES:
-                permute_for(r + 1)
-            if ahead:
-                regroup(*ahead)
-            if r == 0:
-                agg_tile(r, 3)
-            else:
-                output_tile(r, 3)
-            if ahead:
-                quantise(*ahead)
+            for m in range(ROW_TILES):
+                dif_tile(r, m)
+            if r + 3 < len(steps):
+                regroup(*steps[r + 3])
+            if r < len(rounds) - 1:
+                for m in range(ROW_TILES):
+                    agg_tile(r, m)
 
         total = psum.tile([P, BANK], F32, tag="dif")
         n_sums = len(rounds) * ROW_TILES
         nc.tensor.matmul(out=total[:, :n_sums], lhsT=ones[:], rhs=square_sums[:], start=True, stop=True)
-        nc.vector.tensor_reduce(
-            out=loss_sum[:], in_=total[:, :n_sums], axis=mybir.AxisListType.X, op=ALU.add
+        nc.vector.tensor_scalar(
+            out=weighted[:],
+            in0=total[:, :n_sums],
+            scalar1=LOSS_WEIGHT,
+            scalar2=0.0,
+            op0=ALU.mult,
+            op1=ALU.add,
+            accum_out=loss[:],
         )
-        nc.vector.tensor_scalar_mul(out=loss[:], in0=loss_sum[:], scalar1=LOSS_WEIGHT)
         loss_out = out_1
         for axis in range(2 - out_1.ndim):
             loss_out = loss_out.unsqueeze(0)

@@ -25,8 +25,8 @@ PLANE_TILES = 2
 R_PAD_WORDS = 48
 
 VECTOR_COLUMNS_HEAD = 320
-VECTOR_COLUMNS = 256
-SCALERS = "gggs"
+VECTOR_COLUMNS = 192
+WARM_UP = 10
 
 THIRD = 1.0 / 3.0
 LOSS_WEIGHT = 0.1 * 0.5 * 2.0
@@ -78,7 +78,7 @@ def tile_sheaflayer_t_e_kernel(tc, F, R_words, R_scales, out_0, out_1):
     with ExitStack() as ctx:
         keep = ctx.enter_context(tc.tile_pool(name="keep", bufs=1))
         stage = ctx.enter_context(tc.tile_pool(name="stage", bufs=3))
-        psum = ctx.enter_context(tc.psum_pool(name="psum", bufs=4))
+        psum = ctx.enter_context(tc.psum_pool(name="psum", bufs=8))
         ctx.enter_context(tc.manual_schedule())
 
         raw_of = {}
@@ -100,11 +100,13 @@ def tile_sheaflayer_t_e_kernel(tc, F, R_words, R_scales, out_0, out_1):
         w_codes = w_codes_padded[:, R_PAD_WORDS:].rearrange("p (g n) -> p g n", g=n_used)
         w_scales = keep.tile([P, PLANE_TILES, FEATURES], U8, align_bytes=256)
         ones = keep.tile([P, P], F32)
+        zeros = keep.tile([P, BANK], BF16)
         square_sums = keep.tile([P, len(rounds) * ROW_TILES], F32)
         weighted = keep.tile([P, len(rounds) * ROW_TILES], F32)
         loss = keep.tile([P, 1], F32)
 
         nc.vector.memset(r_scales[:].bitcast(I32), 0)
+        nc.vector.memset(zeros[:], 0.0)
         nc.vector.memset(ones[:], 1.0)
 
         loaded = set()
@@ -139,12 +141,12 @@ def tile_sheaflayer_t_e_kernel(tc, F, R_words, R_scales, out_0, out_1):
             )
 
         load_raw(0, 0)
-        load_raw(0, 1)
         load_weights(group(0, 1))
+        load_raw(0, 1)
         load_weights(group(1, 0))
-        load_raw(0, 2)
         load_weights(group(0, 2))
         load_weights(group(1, 2))
+        load_raw(0, 2)
         load_raw(1, 0)
         load_weights(group(2, 0))
         load_weights(group(2, 1))
@@ -184,9 +186,24 @@ def tile_sheaflayer_t_e_kernel(tc, F, R_words, R_scales, out_0, out_1):
                     in_=values,
                 )
 
+        def third_of_residual(r):
+            bank, left_out = rounds[r]
+            cols = slice(bank * BANK, (bank + 1) * BANK)
+            first, end = span_of(bank, RAW_SPANS)
+            start = bank * BANK - first
+            for m in range(ROW_TILES):
+                nc.gpsimd.tensor_scalar(
+                    out=result[:, left_out, m, cols],
+                    in0=raw_of[(left_out, first)][:, m, start : start + BANK],
+                    scalar1=THIRD,
+                    scalar2=0.0,
+                    op0=ALU.mult,
+                    op1=ALU.add,
+                )
+
         def permute_scales():
             for t in range(PACK):
-                nc.vector.tensor_copy(
+                nc.gpsimd.tensor_copy(
                     out=w_scales[:, :, t * P : (t + 1) * P],
                     in_=r_scales[:, :, t:FEATURES:PACK],
                 )
@@ -198,9 +215,11 @@ def tile_sheaflayer_t_e_kernel(tc, F, R_words, R_scales, out_0, out_1):
                 in_=r_codes[:, g, :].bitcast(I32).rearrange("p (m t) -> p t m", t=PACK),
             )
 
-        def two_passes(acc, m, cols, terms, codes, scales):
+        def passes(acc, m, cols, terms, codes, scales, which):
             rows = slice(m * P, (m + 1) * P)
             for n, (e, v) in enumerate(terms):
+                if n not in which:
+                    continue
                 nc.tensor.matmul_mx(
                     out=acc[:],
                     lhsT=codes[:, used_groups.index(e), rows].bitcast(FP8X4),
@@ -211,15 +230,27 @@ def tile_sheaflayer_t_e_kernel(tc, F, R_words, R_scales, out_0, out_1):
                     stop=(n == len(terms) - 1),
                 )
 
-        def dif_tile(r, m):
+        open_groups = {}
+
+        def dif_tile(r, m, which=(0, 1)):
             bank, left_out = rounds[r]
             i, j = others(left_out)
             cols = slice(bank * BANK, (bank + 1) * BANK)
 
-            dif = psum.tile([P, BANK], F32)
-            two_passes(
-                dif, m, cols, ((group(i, j), plus(i)), (group(j, i), minus(j))), r_codes, r_scales
+            if 0 in which:
+                open_groups[("dif", r, m)] = psum.tile([P, BANK], F32, name="dif", tag="acc")
+            dif = open_groups[("dif", r, m)]
+            passes(
+                dif,
+                m,
+                cols,
+                ((group(i, j), plus(i)), (group(j, i), minus(j))),
+                r_codes,
+                r_scales,
+                which,
             )
+            if 1 not in which:
+                return
             squares = stage.tile([P, BANK], BF16)
             nc.scalar.activation(
                 out=squares[:],
@@ -228,39 +259,33 @@ def tile_sheaflayer_t_e_kernel(tc, F, R_words, R_scales, out_0, out_1):
                 accum_out=square_sums[:, r * ROW_TILES + m : r * ROW_TILES + m + 1],
             )
 
-        def agg_tile(r, m):
+        def agg_tile(r, m, which=(0, 1)):
             bank, left_out = rounds[r]
             i, j = others(left_out)
             cols = slice(bank * BANK, (bank + 1) * BANK)
 
-            agg = psum.tile([P, BANK], F32)
-            two_passes(
+            if 0 in which:
+                open_groups[("agg", r, m)] = psum.tile([P, BANK], F32, name="agg", tag="acc")
+            agg = open_groups[("agg", r, m)]
+            passes(
                 agg,
                 m,
                 cols,
                 ((group(i, left_out), plus(i)), (group(j, left_out), plus(j))),
                 w_codes,
                 w_scales,
+                which,
             )
-            first, end = span_of(bank, RAW_SPANS)
-            start = bank * BANK - first
-            nc.vector.tensor_tensor(
+            if 1 not in which:
+                return
+            nc.vector.scalar_tensor_tensor(
                 out=result[:, left_out, m, cols],
                 in0=agg[:],
-                in1=raw_of[(left_out, first)][:, m, start : start + BANK],
-                op=ALU.add,
+                scalar=THIRD,
+                in1=result[:, left_out, m, cols],
+                op0=ALU.mult,
+                op1=ALU.add,
             )
-            if SCALERS[m] == "g":
-                nc.gpsimd.tensor_scalar(
-                    out=result[:, left_out, m, cols],
-                    in0=result[:, left_out, m, cols],
-                    scalar1=THIRD,
-                    scalar2=0.0,
-                    op0=ALU.mult,
-                    op1=ALU.add,
-                )
-            else:
-                nc.scalar.mul(result[:, left_out, m, cols], result[:, left_out, m, cols], THIRD)
             first, end = span_of(bank, STORE_SPANS)
             if (bank + 1) * BANK == end:
                 nc.sync.dma_start(
@@ -268,35 +293,58 @@ def tile_sheaflayer_t_e_kernel(tc, F, R_words, R_scales, out_0, out_1):
                     in_=result[:, left_out, m, first:end],
                 )
 
-        def permute_for(r, engine):
-            bank, left_out = rounds[r]
-            for i in others(left_out):
-                permute_codes(group(i, left_out), engine)
-
+        warm = psum.tile([P, BANK], F32, tag="acc")
+        for n in range(WARM_UP):
+            nc.tensor.matmul(out=warm[:], lhsT=zeros[:, :P], rhs=zeros[:], start=True, stop=True)
         regroup(*steps[0])
-        regroup(*steps[1])
         quantise(*steps[0])
+        regroup(*steps[1])
         quantise(*steps[1])
-        permute_scales()
-        permute_for(0, nc.vector)
+        permute_codes(group(1, 2), nc.vector)
         regroup(*steps[2])
-        permute_for(1, nc.gpsimd)
-        permute_for(2, nc.gpsimd)
-        for r in range(len(rounds)):
+        permute_codes(group(0, 1), nc.gpsimd)
+        permute_codes(group(1, 0), nc.gpsimd)
+        permute_codes(group(0, 2), nc.gpsimd)
+        permute_scales()
+        third_of_residual(0)
+        permute_codes(group(2, 1), nc.gpsimd)
+        permute_codes(group(2, 0), nc.gpsimd)
+        for r in range(1, len(rounds)):
+            third_of_residual(r)
+        for m in range(ROW_TILES):
+            dif_tile(0, m, (0,))
+        for m in range(ROW_TILES):
+            dif_tile(1, m, (0,))
+        for m in range(ROW_TILES):
+            dif_tile(0, m, (1,))
+        quantise(*steps[2])
+        agg_tile(0, 0)
+        agg_tile(0, 1)
+        regroup(*steps[3])
+        agg_tile(0, 2)
+        agg_tile(0, 3)
+        quantise(*steps[3])
+        for m in range(ROW_TILES):
+            dif_tile(1, m, (1,))
+        regroup(*steps[4])
+        for m in range(ROW_TILES):
+            agg_tile(1, m)
+        for r in range(2, len(rounds)):
             if r + 2 < len(steps):
                 quantise(*steps[r + 2])
             if r == len(rounds) - 1:
                 for m in range(ROW_TILES):
+                    dif_tile(r, m)
                     agg_tile(r, m)
-            for m in range(ROW_TILES):
-                dif_tile(r, m)
-            if r + 3 < len(steps):
-                regroup(*steps[r + 3])
-            if r < len(rounds) - 1:
+            else:
+                for m in range(ROW_TILES):
+                    dif_tile(r, m)
+                if r + 3 < len(steps):
+                    regroup(*steps[r + 3])
                 for m in range(ROW_TILES):
                     agg_tile(r, m)
 
-        total = psum.tile([P, BANK], F32, tag="dif")
+        total = psum.tile([P, BANK], F32, tag="acc")
         n_sums = len(rounds) * ROW_TILES
         nc.tensor.matmul(out=total[:, :n_sums], lhsT=ones[:], rhs=square_sums[:], start=True, stop=True)
         nc.vector.tensor_scalar(

@@ -96,9 +96,12 @@ def tile_sheaflayer_t_e_kernel(tc, F, R_words, R_scales, out_0, out_1):
         r_codes_padded = keep.tile([P, R_PAD_WORDS + n_used * FEATURES], U32, align_bytes=256)
         r_codes = r_codes_padded[:, R_PAD_WORDS:].rearrange("p (g n) -> p g n", g=n_used)
         r_scales = keep.tile([P, PLANE_TILES, FEATURES], U8, align_bytes=256)
-        w_codes_padded = keep.tile([P, R_PAD_WORDS + n_used * FEATURES], U32, align_bytes=256)
-        w_codes = w_codes_padded[:, R_PAD_WORDS:].rearrange("p (g n) -> p g n", g=n_used)
-        w_scales = keep.tile([P, PLANE_TILES, FEATURES], U8, align_bytes=256)
+        resid_of = {}
+        for i in range(PATCHES):
+            for bank in range(BANKS):
+                resid_of[(i, bank)] = keep.tile(
+                    [P, ROW_TILES, BANK], BF16, name="resid_%d_%d" % (i, bank)
+                )
         ones = keep.tile([P, P], F32)
         zeros = keep.tile([P, BANK], BF16)
         square_sums = keep.tile([P, len(rounds) * ROW_TILES], F32)
@@ -140,6 +143,12 @@ def tile_sheaflayer_t_e_kernel(tc, F, R_words, R_scales, out_0, out_1):
                 R_words[e].rearrange("p n t -> p (n t)").bitcast(I32),
             )
 
+        def load_residual(bank, i):
+            nc.sync.dma_start(
+                out=resid_of[(i, bank)][:],
+                in_=F[i, :, bank * BANK : (bank + 1) * BANK].rearrange("(m p) b -> p m b", p=P),
+            )
+
         load_raw(0, 0)
         load_weights(group(0, 1))
         load_raw(0, 1)
@@ -147,11 +156,13 @@ def tile_sheaflayer_t_e_kernel(tc, F, R_words, R_scales, out_0, out_1):
         load_weights(group(0, 2))
         load_weights(group(1, 2))
         load_raw(0, 2)
-        load_raw(1, 0)
+        load_residual(*rounds[0])
         load_weights(group(2, 0))
         load_weights(group(2, 1))
-        for bank, i in steps:
-            load_raw(bank, i)
+        for r in range(1, len(rounds)):
+            if r + 2 < len(steps):
+                load_raw(*steps[r + 2])
+            load_residual(*rounds[r])
 
         grouped_of = {}
 
@@ -189,31 +200,15 @@ def tile_sheaflayer_t_e_kernel(tc, F, R_words, R_scales, out_0, out_1):
         def third_of_residual(r):
             bank, left_out = rounds[r]
             cols = slice(bank * BANK, (bank + 1) * BANK)
-            first, end = span_of(bank, RAW_SPANS)
-            start = bank * BANK - first
             for m in range(ROW_TILES):
                 nc.gpsimd.tensor_scalar(
                     out=result[:, left_out, m, cols],
-                    in0=raw_of[(left_out, first)][:, m, start : start + BANK],
+                    in0=resid_of[(left_out, bank)][:, m, :],
                     scalar1=THIRD,
                     scalar2=0.0,
                     op0=ALU.mult,
                     op1=ALU.add,
                 )
-
-        def permute_scales():
-            for t in range(PACK):
-                nc.gpsimd.tensor_copy(
-                    out=w_scales[:, :, t * P : (t + 1) * P],
-                    in_=r_scales[:, :, t:FEATURES:PACK],
-                )
-
-        def permute_codes(e, engine):
-            g = used_groups.index(e)
-            engine.tensor_copy(
-                out=w_codes[:, g, :].bitcast(I32).rearrange("p (t m) -> p t m", t=PACK),
-                in_=r_codes[:, g, :].bitcast(I32).rearrange("p (m t) -> p t m", t=PACK),
-            )
 
         def passes(acc, m, cols, terms, codes, scales, which):
             rows = slice(m * P, (m + 1) * P)
@@ -272,8 +267,8 @@ def tile_sheaflayer_t_e_kernel(tc, F, R_words, R_scales, out_0, out_1):
                 m,
                 cols,
                 ((group(i, left_out), plus(i)), (group(j, left_out), plus(j))),
-                w_codes,
-                w_scales,
+                r_codes,
+                r_scales,
                 which,
             )
             if 1 not in which:
@@ -289,7 +284,7 @@ def tile_sheaflayer_t_e_kernel(tc, F, R_words, R_scales, out_0, out_1):
             first, end = span_of(bank, STORE_SPANS)
             if (bank + 1) * BANK == end:
                 nc.sync.dma_start(
-                    out=out_0[left_out].rearrange("(p t) b -> p t b", t=PACK)[:, m, first:end],
+                    out=out_0[left_out, m * P : (m + 1) * P, first:end],
                     in_=result[:, left_out, m, first:end],
                 )
 
@@ -300,16 +295,8 @@ def tile_sheaflayer_t_e_kernel(tc, F, R_words, R_scales, out_0, out_1):
         quantise(*steps[0])
         regroup(*steps[1])
         quantise(*steps[1])
-        permute_codes(group(1, 2), nc.vector)
         regroup(*steps[2])
-        permute_codes(group(0, 1), nc.gpsimd)
-        permute_codes(group(1, 0), nc.gpsimd)
-        permute_codes(group(0, 2), nc.gpsimd)
-        permute_scales()
-        third_of_residual(0)
-        permute_codes(group(2, 1), nc.gpsimd)
-        permute_codes(group(2, 0), nc.gpsimd)
-        for r in range(1, len(rounds)):
+        for r in range(len(rounds)):
             third_of_residual(r)
         for m in range(ROW_TILES):
             dif_tile(0, m, (0,))

@@ -25,7 +25,7 @@ PLANE_TILES = 2
 R_PAD_WORDS = 48
 
 VECTOR_COLUMNS_HEAD = 320
-VECTOR_COLUMNS = 192
+VECTOR_COLUMNS = 128
 WARM_UP = 10
 
 THIRD = 1.0 / 3.0

@@ -25,7 +25,7 @@ PLANE_TILES = 2
 R_PAD_WORDS = 48
 
 VECTOR_COLUMNS_HEAD = 320
-VECTOR_COLUMNS = 128
+VECTOR_COLUMNS = 224
 WARM_UP = 10
 
 THIRD = 1.0 / 3.0
@@ -197,10 +197,16 @@ def tile_sheaflayer_t_e_kernel(tc, F, R_words, R_scales, out_0, out_1):
                     in_=values,
                 )
 
+        def third_on_scalar(r):
+            bank, left_out = rounds[r]
+            cols = slice(bank * BANK, (bank + 1) * BANK)
+            m = ROW_TILES - 1
+            nc.scalar.mul(result[:, left_out, m, cols], resid_of[(left_out, bank)][:, m, :], THIRD)
+
         def third_of_residual(r):
             bank, left_out = rounds[r]
             cols = slice(bank * BANK, (bank + 1) * BANK)
-            for m in range(ROW_TILES):
+            for m in range(ROW_TILES - 1):
                 nc.gpsimd.tensor_scalar(
                     out=result[:, left_out, m, cols],
                     in0=resid_of[(left_out, bank)][:, m, :],
@@ -304,6 +310,7 @@ def tile_sheaflayer_t_e_kernel(tc, F, R_words, R_scales, out_0, out_1):
             dif_tile(1, m, (0,))
         for m in range(ROW_TILES):
             dif_tile(0, m, (1,))
+        third_on_scalar(0)
         quantise(*steps[2])
         agg_tile(0, 0)
         agg_tile(0, 1)
@@ -313,6 +320,7 @@ def tile_sheaflayer_t_e_kernel(tc, F, R_words, R_scales, out_0, out_1):
         quantise(*steps[3])
         for m in range(ROW_TILES):
             dif_tile(1, m, (1,))
+        third_on_scalar(1)
         regroup(*steps[4])
         for m in range(ROW_TILES):
             agg_tile(1, m)
@@ -320,12 +328,14 @@ def tile_sheaflayer_t_e_kernel(tc, F, R_words, R_scales, out_0, out_1):
             if r + 2 < len(steps):
                 quantise(*steps[r + 2])
             if r == len(rounds) - 1:
+                third_on_scalar(r)
                 for m in range(ROW_TILES):
                     dif_tile(r, m)
                     agg_tile(r, m)
             else:
                 for m in range(ROW_TILES):
                     dif_tile(r, m)
+                third_on_scalar(r)
                 if r + 3 < len(steps):
                     regroup(*steps[r + 3])
                 for m in range(ROW_TILES):

@@ -166,36 +166,69 @@ def tile_sheaflayer_t_e_kernel(tc, F, R_words, R_scales, out_0, out_1):
 
         grouped_of = {}
 
-        def regroup(bank, i):
+        def new_grouped(bank, i):
             grouped = stage.tile([P, BANK, PACK], BF16, align_bytes=64)
             grouped_of[(bank, i)] = grouped
+            return grouped
+
+        def share(bank, i):
             half = VECTOR_COLUMNS_HEAD if bank == 0 else VECTOR_COLUMNS
             first, end = span_of(bank, RAW_SPANS)
-            raw = raw_of[(i, first)]
-            start = bank * BANK - first
+            return half, raw_of[(i, first)], bank * BANK - first
+
+        def regroup_on_vector(bank, i):
+            grouped = new_grouped(bank, i)
+            half, raw, start = share(bank, i)
             nc.vector.tensor_copy(
                 out=grouped[:, :half, :].rearrange("p (c r) t -> p c t r", r=4),
                 in_=raw[:, :, start : start + half].rearrange("p t (c r) -> p c t r", r=4),
             )
+
+        def regroup_on_scalar(bank, i):
+            grouped = grouped_of[(bank, i)]
+            half, raw, start = share(bank, i)
             nc.scalar.copy(
                 out=grouped[:, half:, :].rearrange("p (c r) t -> p c t r", r=4),
                 in_=raw[:, :, start + half : start + BANK].rearrange("p t (c r) -> p c t r", r=4),
             )
 
-        def quantise(bank, i):
+        def regroup(bank, i):
+            regroup_on_vector(bank, i)
+            regroup_on_scalar(bank, i)
+
+        def flat(tile):
+            return tile[:].rearrange("p w t -> p (w t)")
+
+        negated_of = {}
+
+        def negate(bank, i):
+            if i == 0:
+                return
+            negated = stage.tile([P, BANK, PACK], BF16, align_bytes=64)
+            negated_of[(bank, i)] = negated
+            nc.vector.tensor_scalar_mul(
+                out=flat(negated), in0=flat(grouped_of[(bank, i)]), scalar1=-1.0
+            )
+
+        def quantise_as(v, bank, values):
             cols = slice(bank * BANK, (bank + 1) * BANK)
-            positive = grouped_of[(bank, i)][:].rearrange("p w t -> p (w t)")
-            signed = [(plus(i), positive)]
+            nc.vector.quantize_mx(
+                out=f_codes[:, v, cols].bitcast(FP8X4),
+                scales=f_scales[:, v, cols],
+                in_=flat(values),
+            )
+
+        def quantise_plus(bank, i):
+            quantise_as(plus(i), bank, grouped_of[(bank, i)])
+
+        def quantise_minus(bank, i):
             if i > 0:
-                negated = stage.tile([P, BANK * PACK], BF16, align_bytes=64)
-                nc.vector.tensor_scalar_mul(out=negated[:], in0=positive, scalar1=-1.0)
-                signed = [(minus(i), negated[:]), (plus(i), positive)]
-            for v, values in signed:
-                nc.vector.quantize_mx(
-                    out=f_codes[:, v, cols].bitcast(FP8X4),
-                    scales=f_scales[:, v, cols],
-                    in_=values,
-                )
+                quantise_as(minus(i), bank, negated_of[(bank, i)])
+
+        def quantise(bank, i):
+            negate(bank, i)
+            quantise_minus(bank, i)
+            quantise_plus(bank, i)
 
         def third_on_scalar(r):
             bank, left_out = rounds[r]
@@ -326,7 +359,12 @@ def tile_sheaflayer_t_e_kernel(tc, F, R_words, R_scales, out_0, out_1):
             agg_tile(1, m)
         for r in range(2, len(rounds)):
             if r + 2 < len(steps):
-                quantise(*steps[r + 2])
+                negate(*steps[r + 2])
+                quantise_plus(*steps[r + 2])
+            if r + 3 < len(steps):
+                regroup_on_vector(*steps[r + 3])
+            if r + 2 < len(steps):
+                quantise_minus(*steps[r + 2])
             if r == len(rounds) - 1:
                 third_on_scalar(r)
                 for m in range(ROW_TILES):
@@ -337,7 +375,7 @@ def tile_sheaflayer_t_e_kernel(tc, F, R_words, R_scales, out_0, out_1):
                     dif_tile(r, m)
                 third_on_scalar(r)
                 if r + 3 < len(steps):
-                    regroup(*steps[r + 3])
+                    regroup_on_scalar(*steps[r + 3])
                 for m in range(ROW_TILES):
                     agg_tile(r, m)
 

@@ -24,14 +24,14 @@ PLANES = 4
 PLANE_TILES = 2
 R_PAD_WORDS = 48
 
-VECTOR_COLUMNS_HEAD = 320
-VECTOR_COLUMNS = 224
+VECTOR_COLUMNS = (320, 320, 416, 160, 160, 160, 160, 160, 160)
 WARM_UP = 10
 
 THIRD = 1.0 / 3.0
 LOSS_WEIGHT = 0.1 * 0.5 * 2.0
 
-RAW_SPANS = ((0, 1), (1, 2), (2, 3))
+RAW_SPANS = (((0, 1), (1, 2), (2, 3)), ((0, 1), (1, 2), (2, 3)), ((0, 1), (1, 3)))
+RESID_SPANS = (((0, 1), (1, 3)),) * 3
 STORE_SPANS = ((0, 2), (2, 3))
 
 FLOPS = 2 * FEATURES * FEATURES * COLUMNS * 2 * PATCHES * (PATCHES - 1)
@@ -84,7 +84,7 @@ def tile_sheaflayer_t_e_kernel(tc, F, R_words, R_scales, out_0, out_1):
         raw_of = {}
         for i in range(PATCHES):
             for bank in range(BANKS):
-                first, end = span_of(bank, RAW_SPANS)
+                first, end = span_of(bank, RAW_SPANS[i])
                 if first == bank * BANK:
                     raw_of[(i, first)] = keep.tile(
                         [P, PACK, end - first], BF16, name="raw_%d_%d" % (i, first)
@@ -99,9 +99,11 @@ def tile_sheaflayer_t_e_kernel(tc, F, R_words, R_scales, out_0, out_1):
         resid_of = {}
         for i in range(PATCHES):
             for bank in range(BANKS):
-                resid_of[(i, bank)] = keep.tile(
-                    [P, ROW_TILES, BANK], BF16, name="resid_%d_%d" % (i, bank)
-                )
+                first, end = span_of(bank, RESID_SPANS[i])
+                if first == bank * BANK:
+                    resid_of[(i, first)] = keep.tile(
+                        [P, ROW_TILES, end - first], BF16, name="resid_%d_%d" % (i, first)
+                    )
         ones = keep.tile([P, P], F32)
         zeros = keep.tile([P, BANK], BF16)
         square_sums = keep.tile([P, len(rounds) * ROW_TILES], F32)
@@ -120,14 +122,14 @@ def tile_sheaflayer_t_e_kernel(tc, F, R_words, R_scales, out_0, out_1):
                 nc.sync.dma_start(out=out, in_=in_)
 
         def load_raw(bank, i):
-            first, end = span_of(bank, RAW_SPANS)
+            first, end = span_of(bank, RAW_SPANS[i])
             load_once(
                 ("raw", i, first),
                 raw_of[(i, first)][:],
                 F[i, :, first:end].rearrange("(p t) b -> p t b", t=PACK),
             )
 
-        def load_weights(e):
+        def load_scales(e):
             h = e // PLANES
             for quadrant in range(4):
                 load_once(
@@ -137,6 +139,10 @@ def tile_sheaflayer_t_e_kernel(tc, F, R_words, R_scales, out_0, out_1):
                         PLANES * h : PLANES * (h + 1), 4 * quadrant : 4 * quadrant + 4, :
                     ].bitcast(I32),
                 )
+
+        def load_weights(i, j):
+            e = group(i, j)
+            load_scales(e)
             load_once(
                 ("codes", e),
                 r_codes[:, used_groups.index(e), :].bitcast(I32),
@@ -144,73 +150,74 @@ def tile_sheaflayer_t_e_kernel(tc, F, R_words, R_scales, out_0, out_1):
             )
 
         def load_residual(bank, i):
-            nc.sync.dma_start(
-                out=resid_of[(i, bank)][:],
-                in_=F[i, :, bank * BANK : (bank + 1) * BANK].rearrange("(m p) b -> p m b", p=P),
+            first, end = span_of(bank, RESID_SPANS[i])
+            load_once(
+                ("resid", i, first),
+                resid_of[(i, first)][:],
+                F[i, :, first:end].rearrange("(m p) b -> p m b", p=P),
             )
 
+        def residual(r, m):
+            bank, left_out = rounds[r]
+            first, end = span_of(bank, RESID_SPANS[left_out])
+            return resid_of[(left_out, first)][:, m, bank * BANK - first : (bank + 1) * BANK - first]
+
         load_raw(0, 0)
-        load_weights(group(0, 1))
+        load_weights(0, 1)
         load_raw(0, 1)
-        load_weights(group(1, 0))
-        load_weights(group(0, 2))
-        load_weights(group(1, 2))
+        load_weights(0, 2)
+        load_weights(1, 0)
         load_raw(0, 2)
-        load_residual(*rounds[0])
-        load_weights(group(2, 0))
-        load_weights(group(2, 1))
+        load_weights(1, 2)
+        load_residual(0, 2)
+        load_weights(2, 0)
+        load_weights(2, 1)
         for r in range(1, len(rounds)):
             if r + 2 < len(steps):
                 load_raw(*steps[r + 2])
             load_residual(*rounds[r])
 
         grouped_of = {}
-
-        def new_grouped(bank, i):
-            grouped = stage.tile([P, BANK, PACK], BF16, align_bytes=64)
-            grouped_of[(bank, i)] = grouped
-            return grouped
-
-        def share(bank, i):
-            half = VECTOR_COLUMNS_HEAD if bank == 0 else VECTOR_COLUMNS
-            first, end = span_of(bank, RAW_SPANS)
-            return half, raw_of[(i, first)], bank * BANK - first
-
-        def regroup_on_vector(bank, i):
-            grouped = new_grouped(bank, i)
-            half, raw, start = share(bank, i)
-            nc.vector.tensor_copy(
-                out=grouped[:, :half, :].rearrange("p (c r) t -> p c t r", r=4),
-                in_=raw[:, :, start : start + half].rearrange("p t (c r) -> p c t r", r=4),
-            )
-
-        def regroup_on_scalar(bank, i):
-            grouped = grouped_of[(bank, i)]
-            half, raw, start = share(bank, i)
-            nc.scalar.copy(
-                out=grouped[:, half:, :].rearrange("p (c r) t -> p c t r", r=4),
-                in_=raw[:, :, start + half : start + BANK].rearrange("p t (c r) -> p c t r", r=4),
-            )
-
-        def regroup(bank, i):
-            regroup_on_vector(bank, i)
-            regroup_on_scalar(bank, i)
+        positive_of = {}
 
         def flat(tile):
             return tile[:].rearrange("p w t -> p (w t)")
 
-        negated_of = {}
-
-        def negate(bank, i):
-            if i == 0:
+        def regroup_part(copy, multiply, step, start, end):
+            if start == end:
                 return
-            negated = stage.tile([P, BANK, PACK], BF16, align_bytes=64)
-            negated_of[(bank, i)] = negated
-            nc.vector.tensor_scalar_mul(
-                out=flat(negated), in0=flat(grouped_of[(bank, i)]), scalar1=-1.0
+            bank, i = steps[step]
+            first, last = span_of(bank, RAW_SPANS[i])
+            skip = bank * BANK - first
+            out = grouped_of[step][:, start:end, :].rearrange("p (c r) t -> p c t r", r=4)
+            in_ = raw_of[(i, first)][:, :, skip + start : skip + end].rearrange(
+                "p t (c r) -> p c t r", r=4
+            )
+            if i == 0:
+                copy(out, in_)
+            else:
+                multiply(out, in_, -1.0)
+
+        def regroup_on_vector(step):
+            grouped = stage.tile([P, BANK, PACK], BF16, align_bytes=64)
+            grouped_of[step] = grouped
+            regroup_part(
+                nc.vector.tensor_copy, nc.vector.tensor_scalar_mul, step, 0, VECTOR_COLUMNS[step]
             )
 
-        def quantise_as(v, bank, values):
+        def regroup_on_scalar(step):
+            regroup_part(nc.scalar.copy, nc.scalar.mul, step, VECTOR_COLUMNS[step], BANK)
+
+        def negate(step):
+            if steps[step][1] > 0:
+                positive = stage.tile([P, BANK, PACK], BF16, align_bytes=64)
+                positive_of[step] = positive
+                nc.vector.tensor_scalar_mul(
+                    out=flat(positive), in0=flat(grouped_of[step]), scalar1=-1.0
+                )
+
+        def quantise_as(v, step, values):
+            bank = steps[step][0]
             cols = slice(bank * BANK, (bank + 1) * BANK)
             nc.vector.quantize_mx(
                 out=f_codes[:, v, cols].bitcast(FP8X4),
@@ -218,108 +225,92 @@ def tile_sheaflayer_t_e_kernel(tc, F, R_words, R_scales, out_0, out_1):
                 in_=flat(values),
             )
 
-        def quantise_plus(bank, i):
-            quantise_as(plus(i), bank, grouped_of[(bank, i)])
+        def quantise_plus(step):
+            quantise_as(
+                plus(steps[step][1]), step, positive_of[step] if steps[step][1] > 0 else grouped_of[step]
+            )
 
-        def quantise_minus(bank, i):
-            if i > 0:
-                quantise_as(minus(i), bank, negated_of[(bank, i)])
+        def quantise_minus(step):
+            if steps[step][1] > 0:
+                quantise_as(minus(steps[step][1]), step, grouped_of[step])
 
-        def quantise(bank, i):
-            negate(bank, i)
-            quantise_minus(bank, i)
-            quantise_plus(bank, i)
+        def columns_of(r):
+            bank = rounds[r][0]
+            return slice(bank * BANK, (bank + 1) * BANK)
 
-        def third_on_scalar(r):
+        def third_on_scalar(r, tiles=(ROW_TILES - 1,)):
             bank, left_out = rounds[r]
-            cols = slice(bank * BANK, (bank + 1) * BANK)
-            m = ROW_TILES - 1
-            nc.scalar.mul(result[:, left_out, m, cols], resid_of[(left_out, bank)][:, m, :], THIRD)
+            for m in tiles:
+                nc.scalar.mul(
+                    result[:, left_out, m, columns_of(r)], residual(r, m), THIRD
+                )
 
-        def third_of_residual(r):
+        def third_on_gpsimd(r, tiles=range(ROW_TILES - 1)):
             bank, left_out = rounds[r]
-            cols = slice(bank * BANK, (bank + 1) * BANK)
-            for m in range(ROW_TILES - 1):
+            for m in tiles:
                 nc.gpsimd.tensor_scalar(
-                    out=result[:, left_out, m, cols],
-                    in0=resid_of[(left_out, bank)][:, m, :],
+                    out=result[:, left_out, m, columns_of(r)],
+                    in0=residual(r, m),
                     scalar1=THIRD,
                     scalar2=0.0,
                     op0=ALU.mult,
                     op1=ALU.add,
                 )
 
-        def passes(acc, m, cols, terms, codes, scales, which):
-            rows = slice(m * P, (m + 1) * P)
-            for n, (e, v) in enumerate(terms):
-                if n not in which:
-                    continue
-                nc.tensor.matmul_mx(
-                    out=acc[:],
-                    lhsT=codes[:, used_groups.index(e), rows].bitcast(FP8X4),
-                    lhsT_scale=scales[4 * (e % PLANES) : P, e // PLANES, rows],
-                    rhs=f_codes[:, v, cols].bitcast(FP8X4),
-                    rhs_scale=f_scales[:, v, cols],
-                    start=(n == 0),
-                    stop=(n == len(terms) - 1),
-                )
-
         open_groups = {}
 
-        def dif_tile(r, m, which=(0, 1)):
-            bank, left_out = rounds[r]
-            i, j = others(left_out)
-            cols = slice(bank * BANK, (bank + 1) * BANK)
-
-            if 0 in which:
-                open_groups[("dif", r, m)] = psum.tile([P, BANK], F32, name="dif", tag="acc")
-            dif = open_groups[("dif", r, m)]
-            passes(
-                dif,
-                m,
-                cols,
-                ((group(i, j), plus(i)), (group(j, i), minus(j))),
-                r_codes,
-                r_scales,
-                which,
+        def product(kind, r, m, e, v, first):
+            if first:
+                open_groups[(kind, r, m)] = psum.tile([P, BANK], F32, name="acc", tag="acc")
+            rows = slice(m * P, (m + 1) * P)
+            nc.tensor.matmul_mx(
+                out=open_groups[(kind, r, m)][:],
+                lhsT=r_codes[:, used_groups.index(e), rows].bitcast(FP8X4),
+                lhsT_scale=r_scales[4 * (e % PLANES) : P, e // PLANES, rows],
+                rhs=f_codes[:, v, columns_of(r)].bitcast(FP8X4),
+                rhs_scale=f_scales[:, v, columns_of(r)],
+                start=first,
+                stop=not first,
             )
-            if 1 not in which:
-                return
+
+        def open_dif(r, m):
+            i, j = others(rounds[r][1])
+            product("dif", r, m, group(i, j), plus(i), True)
+
+        def close_dif(r, m):
+            i, j = others(rounds[r][1])
+            product("dif", r, m, group(j, i), minus(j), False)
+
+        def square(r, m):
             squares = stage.tile([P, BANK], BF16)
             nc.scalar.activation(
                 out=squares[:],
-                in_=dif[:],
+                in_=open_groups[("dif", r, m)][:],
                 func=ACT.Square,
                 accum_out=square_sums[:, r * ROW_TILES + m : r * ROW_TILES + m + 1],
             )
 
-        def agg_tile(r, m, which=(0, 1)):
-            bank, left_out = rounds[r]
+        def open_agg(r, m):
+            left_out = rounds[r][1]
             i, j = others(left_out)
-            cols = slice(bank * BANK, (bank + 1) * BANK)
+            product("agg", r, m, group(i, left_out), plus(i), True)
 
-            if 0 in which:
-                open_groups[("agg", r, m)] = psum.tile([P, BANK], F32, name="agg", tag="acc")
-            agg = open_groups[("agg", r, m)]
-            passes(
-                agg,
-                m,
-                cols,
-                ((group(i, left_out), plus(i)), (group(j, left_out), plus(j))),
-                r_codes,
-                r_scales,
-                which,
-            )
-            if 1 not in which:
-                return
+        def close_agg(r, m):
+            left_out = rounds[r][1]
+            i, j = others(left_out)
+            product("agg", r, m, group(j, left_out), plus(j), False)
+
+        def add_up(r, m):
+            left_out = rounds[r][1]
             nc.vector.scalar_tensor_tensor(
-                out=result[:, left_out, m, cols],
-                in0=agg[:],
+                out=result[:, left_out, m, columns_of(r)],
+                in0=open_groups[("agg", r, m)][:],
                 scalar=THIRD,
-                in1=result[:, left_out, m, cols],
+                in1=result[:, left_out, m, columns_of(r)],
                 op0=ALU.mult,
                 op1=ALU.add,
             )
+            bank = rounds[r][0]
             first, end = span_of(bank, STORE_SPANS)
             if (bank + 1) * BANK == end:
                 nc.sync.dma_start(
@@ -327,56 +318,77 @@ def tile_sheaflayer_t_e_kernel(tc, F, R_words, R_scales, out_0, out_1):
                     in_=result[:, left_out, m, first:end],
                 )
 
+        def dif_tile(r, m):
+            open_dif(r, m)
+            close_dif(r, m)
+            square(r, m)
+
+        def agg_tile(r, m):
+            open_agg(r, m)
+            close_agg(r, m)
+            add_up(r, m)
+
         warm = psum.tile([P, BANK], F32, tag="acc")
         for n in range(WARM_UP):
             nc.tensor.matmul(out=warm[:], lhsT=zeros[:, :P], rhs=zeros[:], start=True, stop=True)
-        regroup(*steps[0])
-        quantise(*steps[0])
-        regroup(*steps[1])
-        quantise(*steps[1])
-        regroup(*steps[2])
+        T4 = range(ROW_TILES)
+        regroup_on_vector(0)
+        regroup_on_scalar(0)
+        quantise_plus(0)
+        regroup_on_vector(1)
+        regroup_on_scalar(1)
+        quantise_minus(1)
+        negate(1)
+        quantise_plus(1)
         for r in range(len(rounds)):
-            third_of_residual(r)
-        for m in range(ROW_TILES):
-            dif_tile(0, m, (0,))
-        for m in range(ROW_TILES):
-            dif_tile(1, m, (0,))
-        for m in range(ROW_TILES):
-            dif_tile(0, m, (1,))
+            third_on_gpsimd(r)
+        for r in (0, 1):
+            for m in T4:
+                open_dif(r, m)
+        regroup_on_vector(2)
+        regroup_on_scalar(2)
+        for m in T4:
+            close_dif(0, m)
+            square(0, m)
         third_on_scalar(0)
-        quantise(*steps[2])
-        agg_tile(0, 0)
-        agg_tile(0, 1)
-        regroup(*steps[3])
-        agg_tile(0, 2)
-        agg_tile(0, 3)
-        quantise(*steps[3])
-        for m in range(ROW_TILES):
-            dif_tile(1, m, (1,))
+        negate(2)
+        quantise_minus(2)
+        quantise_plus(2)
+        for m in T4:
+            agg_tile(0, m)
+        for m in T4:
+            close_dif(1, m)
+            square(1, m)
+        regroup_on_vector(3)
+        regroup_on_scalar(3)
         third_on_scalar(1)
-        regroup(*steps[4])
-        for m in range(ROW_TILES):
+        agg_tile(1, 0)
+        quantise_plus(3)
+        regroup_on_vector(4)
+        regroup_on_scalar(4)
+        for m in (1, 2, 3):
             agg_tile(1, m)
+
         for r in range(2, len(rounds)):
             if r + 2 < len(steps):
-                negate(*steps[r + 2])
-                quantise_plus(*steps[r + 2])
+                quantise_minus(r + 2)
+                negate(r + 2)
             if r + 3 < len(steps):
-                regroup_on_vector(*steps[r + 3])
+                regroup_on_vector(r + 3)
             if r + 2 < len(steps):
-                quantise_minus(*steps[r + 2])
+                quantise_plus(r + 2)
             if r == len(rounds) - 1:
                 third_on_scalar(r)
-                for m in range(ROW_TILES):
+                for m in T4:
                     dif_tile(r, m)
                     agg_tile(r, m)
             else:
-                for m in range(ROW_TILES):
+                for m in T4:
                     dif_tile(r, m)
                 third_on_scalar(r)
                 if r + 3 < len(steps):
-                    regroup_on_scalar(*steps[r + 3])
-                for m in range(ROW_TILES):
+                    regroup_on_scalar(r + 3)
+                for m in T4:
                     agg_tile(r, m)
 
         total = psum.tile([P, BANK], F32, tag="acc")

@@ -24,7 +24,7 @@ PLANES = 4
 PLANE_TILES = 2
 R_PAD_WORDS = 48
 
-VECTOR_COLUMNS = (320, 320, 416, 160, 160, 160, 160, 160, 160)
+VECTOR_COLUMNS = (320, 320, 416, 320, 320, 320, 320, 320, 320)
 WARM_UP = 10
 
 THIRD = 1.0 / 3.0
@@ -332,6 +332,8 @@ def tile_sheaflayer_t_e_kernel(tc, F, R_words, R_scales, out_0, out_1):
         for n in range(WARM_UP):
             nc.tensor.matmul(out=warm[:], lhsT=zeros[:, :P], rhs=zeros[:], start=True, stop=True)
         T4 = range(ROW_TILES)
+        SCALAR_TILES = (2, 3)
+        GPSIMD_TILES = (0, 1)
         regroup_on_vector(0)
         regroup_on_scalar(0)
         quantise_plus(0)
@@ -341,7 +343,7 @@ def tile_sheaflayer_t_e_kernel(tc, F, R_words, R_scales, out_0, out_1):
         negate(1)
         quantise_plus(1)
         for r in range(len(rounds)):
-            third_on_gpsimd(r)
+            third_on_gpsimd(r, GPSIMD_TILES)
         for r in (0, 1):
             for m in T4:
                 open_dif(r, m)
@@ -350,7 +352,8 @@ def tile_sheaflayer_t_e_kernel(tc, F, R_words, R_scales, out_0, out_1):
         for m in T4:
             close_dif(0, m)
             square(0, m)
-        third_on_scalar(0)
+
+        third_on_scalar(0, SCALAR_TILES)
         negate(2)
         quantise_minus(2)
         quantise_plus(2)
@@ -361,14 +364,13 @@ def tile_sheaflayer_t_e_kernel(tc, F, R_words, R_scales, out_0, out_1):
             square(1, m)
         regroup_on_vector(3)
         regroup_on_scalar(3)
-        third_on_scalar(1)
+        third_on_scalar(1, SCALAR_TILES)
         agg_tile(1, 0)
         quantise_plus(3)
         regroup_on_vector(4)
         regroup_on_scalar(4)
         for m in (1, 2, 3):
             agg_tile(1, m)
-
         for r in range(2, len(rounds)):
             if r + 2 < len(steps):
                 quantise_minus(r + 2)
@@ -378,14 +380,14 @@ def tile_sheaflayer_t_e_kernel(tc, F, R_words, R_scales, out_0, out_1):
             if r + 2 < len(steps):
                 quantise_plus(r + 2)
             if r == len(rounds) - 1:
-                third_on_scalar(r)
+                third_on_scalar(r, SCALAR_TILES)
                 for m in T4:
                     dif_tile(r, m)
                     agg_tile(r, m)
             else:
                 for m in T4:
                     dif_tile(r, m)
-                third_on_scalar(r)
+                third_on_scalar(r, SCALAR_TILES)
                 if r + 3 < len(steps):
                     regroup_on_scalar(r + 3)
                 for m in T4:

@@ -24,7 +24,7 @@ PLANES = 4
 PLANE_TILES = 2
 R_PAD_WORDS = 48
 
-VECTOR_COLUMNS = (320, 320, 416, 320, 320, 320, 320, 320, 320)
+VECTOR_COLUMNS = (320, 416, 416, 320, 224, 320, 320, 320, 320)
 WARM_UP = 10
 
 THIRD = 1.0 / 3.0
@@ -343,7 +343,7 @@ def tile_sheaflayer_t_e_kernel(tc, F, R_words, R_scales, out_0, out_1):
         negate(1)
         quantise_plus(1)
         for r in range(len(rounds)):
-            third_on_gpsimd(r, GPSIMD_TILES)
+            third_on_gpsimd(r, (2, 3) if r == 0 else GPSIMD_TILES)
         for r in (0, 1):
             for m in T4:
                 open_dif(r, m)
@@ -353,7 +353,7 @@ def tile_sheaflayer_t_e_kernel(tc, F, R_words, R_scales, out_0, out_1):
             close_dif(0, m)
             square(0, m)
 
-        third_on_scalar(0, SCALAR_TILES)
+        third_on_scalar(0, (0, 1))
         negate(2)
         quantise_minus(2)
         quantise_plus(2)

@@ -24,7 +24,7 @@ PLANES = 4
 PLANE_TILES = 2
 R_PAD_WORDS = 48
 
-VECTOR_COLUMNS = (320, 416, 416, 320, 224, 320, 320, 320, 320)
+VECTOR_COLUMNS = (320, 416, 416, 320, 224, 288, 288, 288, 288)
 WARM_UP = 10
 
 THIRD = 1.0 / 3.0
@@ -169,8 +169,8 @@ def tile_sheaflayer_t_e_kernel(tc, F, R_words, R_scales, out_0, out_1):
         load_weights(1, 0)
         load_raw(0, 2)
         load_weights(1, 2)
-        load_residual(0, 2)
         load_weights(2, 0)
+        load_residual(0, 2)
         load_weights(2, 1)
         for r in range(1, len(rounds)):
             if r + 2 < len(steps):
@@ -300,6 +300,40 @@ def tile_sheaflayer_t_e_kernel(tc, F, R_words, R_scales, out_0, out_1):
             i, j = others(left_out)
             product("agg", r, m, group(j, left_out), plus(j), False)
 
+        def last_sum(r, m, pieces):
+            bank, left_out = rounds[r]
+            i, j = others(left_out)
+            rows = slice(m * P, (m + 1) * P)
+            width = BANK // pieces
+            accs = []
+            for n in range(pieces):
+                piece = slice(bank * BANK + n * width, bank * BANK + (n + 1) * width)
+                acc = psum.tile([P, BANK], F32, name="acc", tag="acc")
+                accs.append((acc, piece))
+                for e, v, first in ((group(i, left_out), plus(i), True), (group(j, left_out), plus(j), False)):
+                    nc.tensor.matmul_mx(
+                        out=acc[:, :width],
+                        lhsT=r_codes[:, used_groups.index(e), rows].bitcast(FP8X4),
+                        lhsT_scale=r_scales[4 * (e % PLANES) : P, e // PLANES, rows],
+                        rhs=f_codes[:, v, piece].bitcast(FP8X4),
+                        rhs_scale=f_scales[:, v, piece],
+                        start=first,
+                        stop=not first,
+                    )
+            for acc, piece in accs:
+                nc.vector.scalar_tensor_tensor(
+                    out=result[:, left_out, m, piece],
+                    in0=acc[:, :width],
+                    scalar=THIRD,
+                    in1=result[:, left_out, m, piece],
+                    op0=ALU.mult,
+                    op1=ALU.add,
+                )
+                nc.sync.dma_start(
+                    out=out_0[left_out, m * P : (m + 1) * P, piece],
+                    in_=result[:, left_out, m, piece],
+                )
+
         def add_up(r, m):
             left_out = rounds[r][1]
             nc.vector.scalar_tensor_tensor(
@@ -381,9 +415,11 @@ def tile_sheaflayer_t_e_kernel(tc, F, R_words, R_scales, out_0, out_1):
                 quantise_plus(r + 2)
             if r == len(rounds) - 1:
                 third_on_scalar(r, SCALAR_TILES)
-                for m in T4:
+                for m in (0, 1, 2):
                     dif_tile(r, m)
                     agg_tile(r, m)
+                dif_tile(r, 3)
+                last_sum(r, 3, 2)
             else:
                 for m in T4:
                     dif_tile(r, m)

from contextlib import ExitStack

import concourse.mybir as mybir

BF16 = mybir.dt.bfloat16
F32 = mybir.dt.float32
I32 = mybir.dt.int32
U32 = mybir.dt.uint32
U8 = mybir.dt.uint8
FP8X4 = mybir.dt.float8_e4m3fn_x4
ALU = mybir.AluOpType
ACT = mybir.ActivationFunctionType

PATCHES = 3
FEATURES = 512
COLUMNS = 1536
P = 128
PACK = 4
BANK = 512
ROW_TILES = FEATURES // P
BANKS = COLUMNS // BANK
SCALE_ROWS = FEATURES // 32
PLANES = 4
PLANE_TILES = 2
R_PAD_WORDS = 48

VECTOR_COLUMNS = (320, 416, 416, 320, 224, 288, 288, 288, 288)
WARM_UP = 10

THIRD = 1.0 / 3.0
LOSS_WEIGHT = 0.1 * 0.5 * 2.0

RAW_SPANS = (((0, 1), (1, 2), (2, 3)), ((0, 1), (1, 2), (2, 3)), ((0, 1), (1, 3)))
RESID_SPANS = (((0, 1), (1, 3)),) * 3
STORE_SPANS = ((0, 2), (2, 3))

FLOPS = 2 * FEATURES * FEATURES * COLUMNS * 2 * PATCHES * (PATCHES - 1)
BYTES = (
    PATCHES * FEATURES * COLUMNS * (2 + 4)
    + PATCHES * (PATCHES - 1) * (FEATURES * FEATURES + SCALE_ROWS * FEATURES)
    + 4
)


def plus(i):
    return i


def minus(i):
    return PATCHES + i - 1


VERSIONS = 2 * PATCHES - 1


def group(i, j):
    return PATCHES * i + j


def others(left_out):
    return [i for i in range(PATCHES) if i != left_out]


def span_of(bank, spans):
    for first, end in spans:
        if first <= bank < end:
            return first * BANK, end * BANK
    raise ValueError(bank)


def tile_sheaflayer_t_e_kernel(tc, F, R_words, R_scales, out_0, out_1):
    nc = tc.nc
    used_groups = [group(i, j) for i in range(PATCHES) for j in range(PATCHES) if i != j]

    rounds = [(bank, left_out) for bank in range(BANKS) for left_out in (2, 1, 0)]
    steps = [(bank, i) for bank in range(BANKS) for i in range(PATCHES)]

    with ExitStack() as ctx:
        keep = ctx.enter_context(tc.tile_pool(name="keep", bufs=1))
        stage = ctx.enter_context(tc.tile_pool(name="stage", bufs=3))
        psum = ctx.enter_context(tc.psum_pool(name="psum", bufs=8))
        ctx.enter_context(tc.manual_schedule())

        raw_of = {}
        for i in range(PATCHES):
            for bank in range(BANKS):
                first, end = span_of(bank, RAW_SPANS[i])
                if first == bank * BANK:
                    raw_of[(i, first)] = keep.tile(
                        [P, PACK, end - first], BF16, name="raw_%d_%d" % (i, first)
                    )
        result = keep.tile([P, PATCHES, ROW_TILES, COLUMNS], F32)
        f_codes = keep.tile([P, VERSIONS, COLUMNS], U32, align_bytes=256)
        f_scales = keep.tile([P, VERSIONS, COLUMNS], U8, align_bytes=256)
        n_used = len(used_groups)
        r_codes_padded = keep.tile([P, R_PAD_WORDS + n_used * FEATURES], U32, align_bytes=256)
        r_codes = r_codes_padded[:, R_PAD_WORDS:].rearrange("p (g n) -> p g n", g=n_used)
        r_scales = keep.tile([P, PLANE_TILES, FEATURES], U8, align_bytes=256)
        resid_of = {}
        for i in range(PATCHES):
            for bank in range(BANKS):
                first, end = span_of(bank, RESID_SPANS[i])
                if first == bank * BANK:
                    resid_of[(i, first)] = keep.tile(
                        [P, ROW_TILES, end - first], BF16, name="resid_%d_%d" % (i, first)
                    )
        ones = keep.tile([P, P], F32)
        zeros = keep.tile([P, BANK], BF16)
        square_sums = keep.tile([P, len(rounds) * ROW_TILES], F32)
        weighted = keep.tile([P, len(rounds) * ROW_TILES], F32)
        loss = keep.tile([P, 1], F32)

        nc.vector.memset(r_scales[:].bitcast(I32), 0)
        nc.vector.memset(zeros[:], 0.0)
        nc.vector.memset(ones[:], 1.0)

        loaded = set()

        def load_once(key, out, in_):
            if key not in loaded:
                loaded.add(key)
                nc.sync.dma_start(out=out, in_=in_)

        def load_raw(bank, i):
            first, end = span_of(bank, RAW_SPANS[i])
            load_once(
                ("raw", i, first),
                raw_of[(i, first)][:],
                F[i, :, first:end].rearrange("(p t) b -> p t b", t=PACK),
            )

        def load_scales(e):
            h = e // PLANES
            for quadrant in range(4):
                load_once(
                    ("scales", h, quadrant),
                    r_scales[32 * quadrant : 32 * quadrant + 4 * PLANES, h, :].bitcast(I32),
                    R_scales[
                        PLANES * h : PLANES * (h + 1), 4 * quadrant : 4 * quadrant + 4, :
                    ].bitcast(I32),
                )

        def load_weights(i, j):
            e = group(i, j)
            load_scales(e)
            load_once(
                ("codes", e),
                r_codes[:, used_groups.index(e), :].bitcast(I32),
                R_words[e].rearrange("p n t -> p (n t)").bitcast(I32),
            )

        def load_residual(bank, i):
            first, end = span_of(bank, RESID_SPANS[i])
            load_once(
                ("resid", i, first),
                resid_of[(i, first)][:],
                F[i, :, first:end].rearrange("(m p) b -> p m b", p=P),
            )

        def residual(r, m):
            bank, left_out = rounds[r]
            first, end = span_of(bank, RESID_SPANS[left_out])
            return resid_of[(left_out, first)][:, m, bank * BANK - first : (bank + 1) * BANK - first]

        load_raw(0, 0)
        load_weights(0, 1)
        load_raw(0, 1)
        load_weights(0, 2)
        load_weights(1, 0)
        load_raw(0, 2)
        load_weights(1, 2)
        load_weights(2, 0)
        load_residual(0, 2)
        load_weights(2, 1)
        for r in range(1, len(rounds)):
            if r + 2 < len(steps):
                load_raw(*steps[r + 2])
            load_residual(*rounds[r])

        grouped_of = {}
        positive_of = {}

        def flat(tile):
            return tile[:].rearrange("p w t -> p (w t)")

        def regroup_part(copy, multiply, step, start, end):
            if start == end:
                return
            bank, i = steps[step]
            first, last = span_of(bank, RAW_SPANS[i])
            skip = bank * BANK - first
            out = grouped_of[step][:, start:end, :].rearrange("p (c r) t -> p c t r", r=4)
            in_ = raw_of[(i, first)][:, :, skip + start : skip + end].rearrange(
                "p t (c r) -> p c t r", r=4
            )
            if i == 0:
                copy(out, in_)
            else:
                multiply(out, in_, -1.0)

        def regroup_on_vector(step):
            grouped = stage.tile([P, BANK, PACK], BF16, align_bytes=64)
            grouped_of[step] = grouped
            regroup_part(
                nc.vector.tensor_copy, nc.vector.tensor_scalar_mul, step, 0, VECTOR_COLUMNS[step]
            )

        def regroup_on_scalar(step):
            regroup_part(nc.scalar.copy, nc.scalar.mul, step, VECTOR_COLUMNS[step], BANK)

        def negate(step):
            if steps[step][1] > 0:
                positive = stage.tile([P, BANK, PACK], BF16, align_bytes=64)
                positive_of[step] = positive
                nc.vector.tensor_scalar_mul(
                    out=flat(positive), in0=flat(grouped_of[step]), scalar1=-1.0
                )

        def quantise_as(v, step, values):
            bank = steps[step][0]
            cols = slice(bank * BANK, (bank + 1) * BANK)
            nc.vector.quantize_mx(
                out=f_codes[:, v, cols].bitcast(FP8X4),
                scales=f_scales[:, v, cols],
                in_=flat(values),
            )

        def quantise_plus(step):
            quantise_as(
                plus(steps[step][1]), step, positive_of[step] if steps[step][1] > 0 else grouped_of[step]
            )

        def quantise_minus(step):
            if steps[step][1] > 0:
                quantise_as(minus(steps[step][1]), step, grouped_of[step])

        def columns_of(r):
            bank = rounds[r][0]
            return slice(bank * BANK, (bank + 1) * BANK)

        def third_on_scalar(r, tiles=(ROW_TILES - 1,)):
            bank, left_out = rounds[r]
            for m in tiles:
                nc.scalar.mul(
                    result[:, left_out, m, columns_of(r)], residual(r, m), THIRD
                )

        def third_on_gpsimd(r, tiles=range(ROW_TILES - 1)):
            bank, left_out = rounds[r]
            for m in tiles:
                nc.gpsimd.tensor_scalar(
                    out=result[:, left_out, m, columns_of(r)],
                    in0=residual(r, m),
                    scalar1=THIRD,
                    scalar2=0.0,
                    op0=ALU.mult,
                    op1=ALU.add,
                )

        open_groups = {}

        def product(kind, r, m, e, v, first):
            if first:
                open_groups[(kind, r, m)] = psum.tile([P, BANK], F32, name="acc", tag="acc")
            rows = slice(m * P, (m + 1) * P)
            nc.tensor.matmul_mx(
                out=open_groups[(kind, r, m)][:],
                lhsT=r_codes[:, used_groups.index(e), rows].bitcast(FP8X4),
                lhsT_scale=r_scales[4 * (e % PLANES) : P, e // PLANES, rows],
                rhs=f_codes[:, v, columns_of(r)].bitcast(FP8X4),
                rhs_scale=f_scales[:, v, columns_of(r)],
                start=first,
                stop=not first,
            )

        def open_dif(r, m):
            i, j = others(rounds[r][1])
            product("dif", r, m, group(i, j), plus(i), True)

        def close_dif(r, m):
            i, j = others(rounds[r][1])
            product("dif", r, m, group(j, i), minus(j), False)

        def square(r, m):
            squares = stage.tile([P, BANK], BF16)
            nc.scalar.activation(
                out=squares[:],
                in_=open_groups[("dif", r, m)][:],
                func=ACT.Square,
                accum_out=square_sums[:, r * ROW_TILES + m : r * ROW_TILES + m + 1],
            )

        def open_agg(r, m):
            left_out = rounds[r][1]
            i, j = others(left_out)
            product("agg", r, m, group(i, left_out), plus(i), True)

        def close_agg(r, m):
            left_out = rounds[r][1]
            i, j = others(left_out)
            product("agg", r, m, group(j, left_out), plus(j), False)

        def last_sum(r, m, pieces):
            bank, left_out = rounds[r]
            i, j = others(left_out)
            rows = slice(m * P, (m + 1) * P)
            width = BANK // pieces
            accs = []
            for n in range(pieces):
                piece = slice(bank * BANK + n * width, bank * BANK + (n + 1) * width)
                acc = psum.tile([P, BANK], F32, name="acc", tag="acc")
                accs.append((acc, piece))
                for e, v, first in ((group(i, left_out), plus(i), True), (group(j, left_out), plus(j), False)):
                    nc.tensor.matmul_mx(
                        out=acc[:, :width],
                        lhsT=r_codes[:, used_groups.index(e), rows].bitcast(FP8X4),
                        lhsT_scale=r_scales[4 * (e % PLANES) : P, e // PLANES, rows],
                        rhs=f_codes[:, v, piece].bitcast(FP8X4),
                        rhs_scale=f_scales[:, v, piece],
                        start=first,
                        stop=not first,
                    )
            for acc, piece in accs:
                nc.vector.scalar_tensor_tensor(
                    out=result[:, left_out, m, piece],
                    in0=acc[:, :width],
                    scalar=THIRD,
                    in1=result[:, left_out, m, piece],
                    op0=ALU.mult,
                    op1=ALU.add,
                )
                nc.sync.dma_start(
                    out=out_0[left_out, m * P : (m + 1) * P, piece],
                    in_=result[:, left_out, m, piece],
                )

        def add_up(r, m):
            left_out = rounds[r][1]
            nc.vector.scalar_tensor_tensor(
                out=result[:, left_out, m, columns_of(r)],
                in0=open_groups[("agg", r, m)][:],
                scalar=THIRD,
                in1=result[:, left_out, m, columns_of(r)],
                op0=ALU.mult,
                op1=ALU.add,
            )
            bank = rounds[r][0]
            first, end = span_of(bank, STORE_SPANS)
            if (bank + 1) * BANK == end:
                nc.sync.dma_start(
                    out=out_0[left_out, m * P : (m + 1) * P, first:end],
                    in_=result[:, left_out, m, first:end],
                )

        def dif_tile(r, m):
            open_dif(r, m)
            close_dif(r, m)
            square(r, m)

        def agg_tile(r, m):
            open_agg(r, m)
            close_agg(r, m)
            add_up(r, m)

        warm = psum.tile([P, BANK], F32, tag="acc")
        for n in range(WARM_UP):
            nc.tensor.matmul(out=warm[:], lhsT=zeros[:, :P], rhs=zeros[:], start=True, stop=True)
        T4 = range(ROW_TILES)
        SCALAR_TILES = (2, 3)
        GPSIMD_TILES = (0, 1)
        regroup_on_vector(0)
        regroup_on_scalar(0)
        quantise_plus(0)
        regroup_on_vector(1)
        regroup_on_scalar(1)
        quantise_minus(1)
        negate(1)
        quantise_plus(1)
        for r in range(len(rounds)):
            third_on_gpsimd(r, (2, 3) if r == 0 else GPSIMD_TILES)
        for r in (0, 1):
            for m in T4:
                open_dif(r, m)
        regroup_on_vector(2)
        regroup_on_scalar(2)
        for m in T4:
            close_dif(0, m)
            square(0, m)

        third_on_scalar(0, (0, 1))
        negate(2)
        quantise_minus(2)
        quantise_plus(2)
        for m in T4:
            agg_tile(0, m)
        for m in T4:
            close_dif(1, m)
            square(1, m)
        regroup_on_vector(3)
        regroup_on_scalar(3)
        third_on_scalar(1, SCALAR_TILES)
        agg_tile(1, 0)
        quantise_plus(3)
        regroup_on_vector(4)
        regroup_on_scalar(4)
        for m in (1, 2, 3):
            agg_tile(1, m)
        for r in range(2, len(rounds)):
            if r + 2 < len(steps):
                quantise_minus(r + 2)
                negate(r + 2)
            if r + 3 < len(steps):
                regroup_on_vector(r + 3)
            if r + 2 < len(steps):
                quantise_plus(r + 2)
            if r == len(rounds) - 1:
                third_on_scalar(r, SCALAR_TILES)
                for m in (0, 1, 2):
                    dif_tile(r, m)
                    agg_tile(r, m)
                dif_tile(r, 3)
                last_sum(r, 3, 2)
            else:
                for m in T4:
                    dif_tile(r, m)
                third_on_scalar(r, SCALAR_TILES)
                if r + 3 < len(steps):
                    regroup_on_scalar(r + 3)
                for m in T4:
                    agg_tile(r, m)

        total = psum.tile([P, BANK], F32, tag="acc")
        n_sums = len(rounds) * ROW_TILES
        nc.tensor.matmul(out=total[:, :n_sums], lhsT=ones[:], rhs=square_sums[:], start=True, stop=True)
        nc.vector.tensor_scalar(
            out=weighted[:],
            in0=total[:, :n_sums],
            scalar1=LOSS_WEIGHT,
            scalar2=0.0,
            op0=ALU.mult,
            op1=ALU.add,
            accum_out=loss[:],
        )
        loss_out = out_1
        for axis in range(2 - out_1.ndim):
            loss_out = loss_out.unsqueeze(0)
        nc.sync.dma_start(out=loss_out, in_=loss[0:1, 0:1])
